import numpy as np
import ml_dtypes


def mxq(x, axis, fmt="e4m3"):
    dtype, down = {"e4m3": (ml_dtypes.float8_e4m3fn, 7), "e5m2": (ml_dtypes.float8_e5m2, 14)}[fmt]
    v = np.moveaxis(np.asarray(x, np.float32).astype(ml_dtypes.bfloat16).astype(np.float64), axis, -1)
    blocks = v.reshape(v.shape[:-1] + (-1, 32))
    amax = np.abs(blocks).max(-1, keepdims=True)
    byte = np.maximum(np.where(amax > 0, np.frexp(amax)[1] - 1 + 127, 0) - down, 1)
    scale = np.exp2(byte - 127.0)
    codes = (blocks / scale).astype(np.float32).astype(dtype).astype(np.float64)
    return np.moveaxis((codes * scale).reshape(v.shape), -1, axis)


WIDE = False


def mx_kscale(k):
    if not WIDE:
        return np.ones(k)
    levels = np.array([10, -10, 5, -5, 0])
    a = np.random.permutation(np.resize(levels, k // 512 * 4)).reshape(k // 512, 4)
    idx = np.arange(k)
    return np.exp2(a[idx // 512, idx % 128 // 32])


BF16 = ml_dtypes.bfloat16


def bf(x):
    return np.asarray(x, np.float32).astype(BF16)


def f64(x):
    return np.asarray(x).astype(np.float64)


B, C, H, W = 1, 512, 64, 32
CH = C // 2
N = H * W
M = (H // 2) * (W // 2)
QS = 1.35 * CH ** -0.25


def pool2(t):
    r = t.reshape(B, -1, H // 2, 2, W // 2, 2)
    return r.max(axis=(3, 5)) + r.mean(axis=(3, 5))


def setup_inputs():
    s = mx_kscale(C)
    s = s / s.max()
    return {"x": bf(np.random.standard_normal((B, C, H, W)) * s[None, :, None, None]),
            "c2": bf(np.random.standard_normal((B, CH, H, W)) * QS),
            "c1p": bf((1.03 + 1.11 * np.random.standard_normal((B, CH, H // 2, W // 2))) * QS),
            "W3": bf(np.random.standard_normal((C, C)) / np.sqrt(C) / s),
            "gamma": bf(1.0 + 0.1 * np.random.standard_normal(1))}


def reference(x, c2, c1p, W3, gamma):
    c3 = mxq(f64(W3), 1, "e4m3") @ mxq(f64(x).reshape(B, C, N), 1, "e4m3")
    c3p = pool2(c3.reshape(B, C, H, W)).reshape(B, C, M)
    sc = f64(c2).reshape(B, CH, N).transpose(0, 2, 1) @ f64(c1p).reshape(B, CH, M)
    e = np.exp(sc - sc.max(-1, keepdims=True))
    num = mxq(c3p, 2, "e4m3") @ mxq(e.transpose(0, 2, 1), 1, "e4m3")
    refined = num / e.sum(-1)[:, None, :]
    return f64(gamma)[0] * refined.reshape(B, C, H, W) + f64(x)

@@ -1,0 +1,181 @@
+from contextlib import ExitStack
+
+import concourse.mybir as mybir
+from concourse.masks import make_identity
+
+F32 = mybir.dt.float32
+BF16 = mybir.dt.bfloat16
+U32 = mybir.dt.uint32
+U8 = mybir.dt.uint8
+FP8X4 = mybir.dt.float8_e4m3fn_x4
+ALU = mybir.AluOpType
+ACTF = mybir.ActivationFunctionType
+AX = mybir.AxisListType
+
+P = 128
+C = 512
+M = 512
+NPIX = 2048
+FLOPS = 2 * (C * C * NPIX + NPIX * M * 256 + C * M * NPIX)
+
+
+def tile_selfspatialattentionmodule_pb_kernel(tc, x, c2, c1p, W3, gamma, out):
+    nc = tc.nc
+    x_v = x[0].rearrange("(p j) h w -> p j (h w)", j=4)
+    out_v = out[0].rearrange("(p j) h w -> p j (h w)", j=4)
+    c2_v = c2[0].rearrange("(g p) h w -> p g (h w)", p=P)
+    c1_v = c1p[0].rearrange("(g p) h w -> p g (h w)", p=P)
+    w3_v = W3.rearrange("(p j) k -> p (j k)", j=4)
+
+    with ExitStack() as ctx:
+        keep = ctx.enter_context(tc.tile_pool(name="keep", bufs=1))
+        epool = ctx.enter_context(tc.tile_pool(name="epool", bufs=3))
+        mpool = ctx.enter_context(tc.tile_pool(name="mpool", bufs=3))
+        tpool = ctx.enter_context(tc.tile_pool(name="tpool", bufs=3))
+        ps_s = ctx.enter_context(tc.psum_pool(name="ps_s", bufs=2))
+        ps_t = ctx.enter_context(tc.psum_pool(name="ps_t", bufs=2))
+        ps_c = ctx.enter_context(tc.psum_pool(name="ps_c", bufs=2))
+        ps_v = ctx.enter_context(tc.psum_pool(name="ps_v", bufs=2))
+
+        c1s = keep.tile([P, 2, M], BF16, name="c1s")
+        c2s = [keep.tile([P, 2, 512], BF16, name="c2s%d" % g) for g in range(4)]
+        xr = [keep.tile([P, 4, 512], BF16, name="xr%d" % g) for g in range(4)]
+        w3r = keep.tile([P, 4 * C], BF16, name="w3r")
+        gam_bf = keep.tile([P, 1], BF16, name="gam_bf")
+
+        def load_c2(g):
+            nc.sync.dma_start(out=c2s[g][:], in_=c2_v[:, :, g * 512:(g + 1) * 512])
+
+        def load_x(g):
+            nc.sync.dma_start(out=xr[g][:], in_=x_v[:, :, g * 512:(g + 1) * 512])
+
+        nc.scalar.dma_start(out=gam_bf[:], in_=gamma.partition_broadcast(P))
+        nc.sync.dma_start(out=c1s[:], in_=c1_v)
+        load_c2(0)
+        nc.sync.dma_start(out=w3r[:], in_=w3_v)
+        load_x(0)
+        load_x(1)
+        load_c2(1)
+        load_x(2)
+        load_x(3)
+        load_c2(2)
+        load_c2(3)
+
+        ident_f = keep.tile([P, P], F32, name="ident_f")
+        make_identity(nc, ident_f[:])
+        ident_bf = keep.tile([P, P], BF16, name="ident_bf")
+        make_identity(nc, ident_bf[:])
+        gam = keep.tile([P, 1], F32, name="gam")
+        nc.vector.tensor_copy(out=gam[:], in_=gam_bf[:])
+
+        w3g = keep.tile([P, 4 * C], BF16, name="w3g", align_bytes=64)
+        w3q = keep.tile([P, C], U32, name="w3q", align_bytes=64)
+        w3s = keep.tile([P, C], U8, name="w3s", align_bytes=64)
+        w3w = w3r[:].bitcast(F32).rearrange("p (j w u) -> p j u w", j=4, w=P, u=2)
+        w3gw = w3g[:].bitcast(F32).rearrange("p (j c u) -> p j c u", j=4, c=P, u=2)
+        for hh in range(2):
+            wt = ps_c.tile([P, 2, 2, P], F32, tag="c", name="wt%d" % hh)
+            for jj in range(2):
+                for u in range(2):
+                    nc.tensor.transpose(wt[:, jj, u, :], w3w[:, 2 * hh + jj, u, :], ident_f[:])
+            src = wt[:].rearrange("p j u c -> p j c u")
+            if hh == 0:
+                nc.vector.tensor_copy(out=w3gw[:, 0:2], in_=src)
+            else:
+                nc.scalar.copy(out=w3gw[:, 2:4], in_=src)
+        nc.vector.quantize_mx(out=w3q[:].bitcast(FP8X4), scales=w3s[:], in_=w3g[:])
+
+        c3p = keep.tile([P, 4, C], BF16, name="c3p")
+        for t in range(4):
+            xg = keep.tile([P, 4, P, 4], BF16, name="xg%d" % t, align_bytes=64)
+            xq = keep.tile([P, 4 * P], U32, name="xq%d" % t, align_bytes=64)
+            xs = keep.tile([P, 4 * P], U8, name="xs%d" % t, align_bytes=64)
+            src = xr[t][:].rearrange("p j (a dh jj dw) -> p dh dw a jj j", a=8, dh=2, jj=16, dw=2)
+            for dh in range(2):
+                nc.vector.tensor_copy(
+                    out=xg[:, 2 * dh:2 * dh + 2].rearrange("p f (a jj) j -> p f a jj j", a=8),
+                    in_=src[:, dh],
+                )
+            nc.vector.quantize_mx(
+                out=xq[:].bitcast(FP8X4), scales=xs[:], in_=xg[:].rearrange("p f c j -> p (f c j)")
+            )
+            sm = ps_v.tile([P, C], F32, tag="v", name="sm%d" % t)
+            mx = None
+            for f in range(4):
+                cols = slice(f * P, (f + 1) * P)
+                bank = ps_c.tile([P, C], F32, tag="c", name="c3_%d_%d" % (t, f))
+                nc.tensor.matmul_mx(
+                    out=bank[:], lhsT=xq[:, cols].bitcast(FP8X4), lhsT_scale=xs[:, cols],
+                    rhs=w3q[:].bitcast(FP8X4), rhs_scale=w3s[:], start=True, stop=True,
+                )
+                nc.tensor.matmul_mx(
+                    out=sm[:], lhsT=xq[:, cols].bitcast(FP8X4), lhsT_scale=xs[:, cols],
+                    rhs=w3q[:].bitcast(FP8X4), rhs_scale=w3s[:], start=(f == 0), stop=(f == 3),
+                )
+                nxt = mpool.tile([P, C], F32, tag="m", name="m_%d_%d" % (t, f))
+                if f == 0:
+                    nc.scalar.copy(out=nxt[:], in_=bank[:])
+                else:
+                    nc.vector.tensor_tensor(out=nxt[:], in0=mx[:], in1=bank[:], op=ALU.max)
+                mx = nxt
+            nc.vector.scalar_tensor_tensor(
+                out=c3p[:, t, :], in0=sm[:], scalar=0.25, in1=mx[:], op0=ALU.mult, op1=ALU.add
+            )
+        c3g = keep.tile([P, C, 4], BF16, name="c3g", align_bytes=64)
+        c3q = keep.tile([P, C], U32, name="c3q", align_bytes=64)
+        c3s = keep.tile([P, C], U8, name="c3s", align_bytes=64)
+        nc.vector.tensor_copy(out=c3g[:], in_=c3p[:].rearrange("p t c -> p c t"))
+        nc.vector.quantize_mx(
+            out=c3q[:].bitcast(FP8X4), scales=c3s[:], in_=c3g[:].rearrange("p c t -> p (c t)")
+        )
+
+        for g in range(4):
+            nmx = keep.tile([P, 4], F32, name="nmx%d" % g)
+            sig = keep.tile([P, 4], F32, name="sig%d" % g)
+            rs = keep.tile([P, 4], F32, name="rs%d" % g)
+            og = keep.tile([P, 4, 512], F32, name="og%d" % g)
+            eqs = []
+            for r in range(4):
+                i = 4 * g + r
+                s = ps_s.tile([P, M], F32, tag="s", name="s%d" % i)
+                for h in range(2):
+                    nc.tensor.matmul(
+                        out=s[:], lhsT=c2s[g][:, h, r * P:(r + 1) * P], rhs=c1s[:, h, :],
+                        start=(h == 0), stop=(h == 1),
+                    )
+                nc.vector.tensor_reduce(out=nmx[:, r:r + 1], in_=s[:], axis=AX.X, op=ALU.max, negate=True)
+                e = epool.tile([P, M], BF16, tag="e", name="e%d" % i)
+                nc.scalar.activation(
+                    out=e[:], in_=s[:], func=ACTF.Exp, bias=nmx[:, r:r + 1], scale=1.0,
+                    accum_out=sig[:, r:r + 1],
+                )
+                et = ps_t.tile([P, 4, P], BF16, tag="t", name="et%d" % i)
+                for t in range(4):
+                    nc.tensor.transpose(et[:, t, :], e[:, t * P:(t + 1) * P], ident_bf[:])
+                eg = keep.tile([P, P, 4], BF16, name="eg%d" % i, align_bytes=64)
+                nc.scalar.copy(out=eg[:], in_=et[:].rearrange("p t n -> p n t"))
+                eq = keep.tile([P, P], U32, name="eq%d" % i, align_bytes=64)
+                es = keep.tile([P, P], U8, name="es%d" % i, align_bytes=64)
+                nc.vector.quantize_mx(
+                    out=eq[:].bitcast(FP8X4), scales=es[:], in_=eg[:].rearrange("p n t -> p (n t)")
+                )
+                eqs.append((eq, es))
+            nc.vector.reciprocal(out=rs[:], in_=sig[:])
+            for r in range(4):
+                i = 4 * g + r
+                eq, es = eqs[r]
+                u = ps_c.tile([P, C], F32, tag="c", name="u%d" % i)
+                nc.tensor.matmul_mx(
+                    out=u[:], lhsT=eq[:].bitcast(FP8X4), lhsT_scale=es[:],
+                    rhs=c3q[:].bitcast(FP8X4), rhs_scale=c3s[:], start=True, stop=True,
+                )
+                tt = tpool.tile([P, C], F32, tag="tt", name="tt%d" % i)
+                nc.scalar.activation(out=tt[:], in_=u[:], func=ACTF.Copy, scale=rs[:, r:r + 1])
+                v = ps_v.tile([P, 4, P], F32, tag="v", name="v%d" % i)
+                for j in range(4):
+                    nc.tensor.transpose(v[:, j, :], tt[:, j * P:(j + 1) * P], ident_f[:])
+                nc.vector.scalar_tensor_tensor(
+                    out=og[:, :, r * P:(r + 1) * P], in0=v[:], scalar=gam[:, 0:1],
+                    in1=xr[g][:, :, r * P:(r + 1) * P], op0=ALU.mult, op1=ALU.add,
+                )
+            nc.sync.dma_start(out=out_v[:, :, g * 512:(g + 1) * 512], in_=og[:])

@@ -16,7 +16,14 @@ P = 128
 C = 512
 M = 512
 NPIX = 2048
+NT = NPIX // P
 FLOPS = 2 * (C * C * NPIX + NPIX * M * 256 + C * M * NPIX)
+
+Q_X = 2
+Q_E = 7
+N_BODIES = 12
+SWITCH = 8
+STORES = ((0, 4), (4, 8), (8, 12), (12, 14), (14, 16))
 
 
 def tile_selfspatialattentionmodule_pb_kernel(tc, x, c2, c1p, W3, gamma, out):
@@ -29,13 +36,14 @@ def tile_selfspatialattentionmodule_pb_kernel(tc, x, c2, c1p, W3, gamma, out):
 
     with ExitStack() as ctx:
         keep = ctx.enter_context(tc.tile_pool(name="keep", bufs=1))
-        epool = ctx.enter_context(tc.tile_pool(name="epool", bufs=3))
-        mpool = ctx.enter_context(tc.tile_pool(name="mpool", bufs=3))
-        tpool = ctx.enter_context(tc.tile_pool(name="tpool", bufs=3))
-        ps_s = ctx.enter_context(tc.psum_pool(name="ps_s", bufs=2))
-        ps_t = ctx.enter_context(tc.psum_pool(name="ps_t", bufs=2))
-        ps_c = ctx.enter_context(tc.psum_pool(name="ps_c", bufs=2))
-        ps_v = ctx.enter_context(tc.psum_pool(name="ps_v", bufs=2))
+        epool = ctx.enter_context(tc.tile_pool(name="epool", bufs=4))
+        mpool = ctx.enter_context(tc.tile_pool(name="mpool", bufs=6))
+        tpool = ctx.enter_context(tc.tile_pool(name="tpool", bufs=4))
+        psum = ctx.enter_context(tc.psum_pool(name="psum", bufs=1))
+        ctx.enter_context(tc.manual_schedule())
+
+        def bank(n, shape, dtype, name):
+            return psum.tile(shape, dtype, tag="bank%d" % n, name=name)
 
         c1s = keep.tile([P, 2, M], BF16, name="c1s")
         c2s = [keep.tile([P, 2, 512], BF16, name="c2s%d" % g) for g in range(4)]
@@ -49,7 +57,6 @@ def tile_selfspatialattentionmodule_pb_kernel(tc, x, c2, c1p, W3, gamma, out):
         def load_x(g):
             nc.sync.dma_start(out=xr[g][:], in_=x_v[:, :, g * 512:(g + 1) * 512])
 
-        nc.scalar.dma_start(out=gam_bf[:], in_=gamma.partition_broadcast(P))
         nc.sync.dma_start(out=c1s[:], in_=c1_v)
         load_c2(0)
         nc.sync.dma_start(out=w3r[:], in_=w3_v)
@@ -60,122 +67,250 @@ def tile_selfspatialattentionmodule_pb_kernel(tc, x, c2, c1p, W3, gamma, out):
         load_x(3)
         load_c2(2)
         load_c2(3)
+        nc.scalar.dma_start(out=gam_bf[:], in_=gamma.partition_broadcast(P))
 
+        warm = keep.tile([P, 1], F32, name="warm")
+        nc.vector.memset(warm[:], 0.0)
+        nc.scalar.activation(out=warm[:], in_=warm[:], func=ACTF.Exp)
         ident_f = keep.tile([P, P], F32, name="ident_f")
         make_identity(nc, ident_f[:])
         ident_bf = keep.tile([P, P], BF16, name="ident_bf")
         make_identity(nc, ident_bf[:])
         gam = keep.tile([P, 1], F32, name="gam")
-        nc.vector.tensor_copy(out=gam[:], in_=gam_bf[:])
 
         w3g = keep.tile([P, 4 * C], BF16, name="w3g", align_bytes=64)
         w3q = keep.tile([P, C], U32, name="w3q", align_bytes=64)
         w3s = keep.tile([P, C], U8, name="w3s", align_bytes=64)
-        w3w = w3r[:].bitcast(F32).rearrange("p (j w u) -> p j u w", j=4, w=P, u=2)
-        w3gw = w3g[:].bitcast(F32).rearrange("p (j c u) -> p j c u", j=4, c=P, u=2)
-        for hh in range(2):
-            wt = ps_c.tile([P, 2, 2, P], F32, tag="c", name="wt%d" % hh)
-            for jj in range(2):
-                for u in range(2):
-                    nc.tensor.transpose(wt[:, jj, u, :], w3w[:, 2 * hh + jj, u, :], ident_f[:])
-            src = wt[:].rearrange("p j u c -> p j c u")
-            if hh == 0:
-                nc.vector.tensor_copy(out=w3gw[:, 0:2], in_=src)
-            else:
-                nc.scalar.copy(out=w3gw[:, 2:4], in_=src)
-        nc.vector.quantize_mx(out=w3q[:].bitcast(FP8X4), scales=w3s[:], in_=w3g[:])
-
-        c3p = keep.tile([P, 4, C], BF16, name="c3p")
-        for t in range(4):
-            xg = keep.tile([P, 4, P, 4], BF16, name="xg%d" % t, align_bytes=64)
-            xq = keep.tile([P, 4 * P], U32, name="xq%d" % t, align_bytes=64)
-            xs = keep.tile([P, 4 * P], U8, name="xs%d" % t, align_bytes=64)
-            src = xr[t][:].rearrange("p j (a dh jj dw) -> p dh dw a jj j", a=8, dh=2, jj=16, dw=2)
-            for dh in range(2):
-                nc.vector.tensor_copy(
-                    out=xg[:, 2 * dh:2 * dh + 2].rearrange("p f (a jj) j -> p f a jj j", a=8),
-                    in_=src[:, dh],
-                )
-            nc.vector.quantize_mx(
-                out=xq[:].bitcast(FP8X4), scales=xs[:], in_=xg[:].rearrange("p f c j -> p (f c j)")
-            )
-            sm = ps_v.tile([P, C], F32, tag="v", name="sm%d" % t)
-            mx = None
-            for f in range(4):
-                cols = slice(f * P, (f + 1) * P)
-                bank = ps_c.tile([P, C], F32, tag="c", name="c3_%d_%d" % (t, f))
-                nc.tensor.matmul_mx(
-                    out=bank[:], lhsT=xq[:, cols].bitcast(FP8X4), lhsT_scale=xs[:, cols],
-                    rhs=w3q[:].bitcast(FP8X4), rhs_scale=w3s[:], start=True, stop=True,
-                )
-                nc.tensor.matmul_mx(
-                    out=sm[:], lhsT=xq[:, cols].bitcast(FP8X4), lhsT_scale=xs[:, cols],
-                    rhs=w3q[:].bitcast(FP8X4), rhs_scale=w3s[:], start=(f == 0), stop=(f == 3),
-                )
-                nxt = mpool.tile([P, C], F32, tag="m", name="m_%d_%d" % (t, f))
-                if f == 0:
-                    nc.scalar.copy(out=nxt[:], in_=bank[:])
-                else:
-                    nc.vector.tensor_tensor(out=nxt[:], in0=mx[:], in1=bank[:], op=ALU.max)
-                mx = nxt
-            nc.vector.scalar_tensor_tensor(
-                out=c3p[:, t, :], in0=sm[:], scalar=0.25, in1=mx[:], op0=ALU.mult, op1=ALU.add
-            )
+        xg = [keep.tile([P, 4, P, 4], BF16, name="xg%d" % t, align_bytes=64) for t in range(4)]
+        xq = [keep.tile([P, 4 * P], U32, name="xq%d" % t, align_bytes=64) for t in range(4)]
+        xs = [keep.tile([P, 4 * P], U8, name="xs%d" % t, align_bytes=64) for t in range(4)]
         c3g = keep.tile([P, C, 4], BF16, name="c3g", align_bytes=64)
         c3q = keep.tile([P, C], U32, name="c3q", align_bytes=64)
         c3s = keep.tile([P, C], U8, name="c3s", align_bytes=64)
-        nc.vector.tensor_copy(out=c3g[:], in_=c3p[:].rearrange("p t c -> p c t"))
-        nc.vector.quantize_mx(
-            out=c3q[:].bitcast(FP8X4), scales=c3s[:], in_=c3g[:].rearrange("p c t -> p (c t)")
-        )
+        eg = [keep.tile([P, P, 4], BF16, name="eg%d" % i, align_bytes=64) for i in range(NT)]
+        eq = [keep.tile([P, P], U32, name="eq%d" % i, align_bytes=64) for i in range(NT)]
+        es = [keep.tile([P, P], U8, name="es%d" % i, align_bytes=64) for i in range(NT)]
+        nmx = [keep.tile([P, 2], F32, name="nmx%d" % i) for i in range(NT // 2)]
+        sig = [keep.tile([P, 2], F32, name="sig%d" % i) for i in range(NT // 2)]
+        rs = [keep.tile([P, 2], F32, name="rs%d" % i) for i in range(NT // 2)]
+        og = [keep.tile([P, 4, (b - a) * P], F32, name="og%d" % a) for (a, b) in STORES]
+        live = {}
 
-        for g in range(4):
-            nmx = keep.tile([P, 4], F32, name="nmx%d" % g)
-            sig = keep.tile([P, 4], F32, name="sig%d" % g)
-            rs = keep.tile([P, 4], F32, name="rs%d" % g)
-            og = keep.tile([P, 4, 512], F32, name="og%d" % g)
-            eqs = []
-            for r in range(4):
-                i = 4 * g + r
-                s = ps_s.tile([P, M], F32, tag="s", name="s%d" % i)
-                for h in range(2):
-                    nc.tensor.matmul(
-                        out=s[:], lhsT=c2s[g][:, h, r * P:(r + 1) * P], rhs=c1s[:, h, :],
-                        start=(h == 0), stop=(h == 1),
-                    )
-                nc.vector.tensor_reduce(out=nmx[:, r:r + 1], in_=s[:], axis=AX.X, op=ALU.max, negate=True)
-                e = epool.tile([P, M], BF16, tag="e", name="e%d" % i)
-                nc.scalar.activation(
-                    out=e[:], in_=s[:], func=ACTF.Exp, bias=nmx[:, r:r + 1], scale=1.0,
-                    accum_out=sig[:, r:r + 1],
+        def ok(i):
+            return 0 <= i < NT
+
+        def regroup_x(t, f, eng):
+            src = xr[t][:].rearrange("p j (a dh jj dw) -> p dh dw a jj j", a=8, dh=2, jj=16, dw=2)
+            dst = xg[t][:, f].rearrange("p (a jj) j -> p a jj j", a=8)
+            if eng == "vector":
+                nc.vector.tensor_copy(out=dst, in_=src[:, f // 2, f % 2])
+            else:
+                nc.gpsimd.tensor_scalar(
+                    out=dst, in0=src[:, f // 2, f % 2], scalar1=1.0, scalar2=0.0,
+                    op0=ALU.mult, op1=ALU.add,
                 )
-                et = ps_t.tile([P, 4, P], BF16, tag="t", name="et%d" % i)
-                for t in range(4):
-                    nc.tensor.transpose(et[:, t, :], e[:, t * P:(t + 1) * P], ident_bf[:])
-                eg = keep.tile([P, P, 4], BF16, name="eg%d" % i, align_bytes=64)
-                nc.scalar.copy(out=eg[:], in_=et[:].rearrange("p t n -> p n t"))
-                eq = keep.tile([P, P], U32, name="eq%d" % i, align_bytes=64)
-                es = keep.tile([P, P], U8, name="es%d" % i, align_bytes=64)
-                nc.vector.quantize_mx(
-                    out=eq[:].bitcast(FP8X4), scales=es[:], in_=eg[:].rearrange("p n t -> p (n t)")
-                )
-                eqs.append((eq, es))
-            nc.vector.reciprocal(out=rs[:], in_=sig[:])
-            for r in range(4):
-                i = 4 * g + r
-                eq, es = eqs[r]
-                u = ps_c.tile([P, C], F32, tag="c", name="u%d" % i)
+
+        def x_engine(t, f):
+            return "vector" if (t == 0 or f == 0) else "gpsimd"
+
+        def regroup_x_on(t, eng):
+            if 0 <= t < 4:
+                for f in range(4):
+                    if x_engine(t, f) == eng:
+                        regroup_x(t, f, eng)
+
+        def quantise_x(t):
+            nc.vector.quantize_mx(
+                out=xq[t][:].bitcast(FP8X4), scales=xs[t][:],
+                in_=xg[t][:].rearrange("p f c j -> p (f c j)"),
+            )
+
+        def w3_transposes():
+            w3w = w3r[:].bitcast(F32).rearrange("p (j w u) -> p j u w", j=4, w=P, u=2)
+            w3gw = w3g[:].bitcast(F32).rearrange("p (j c u) -> p j c u", j=4, c=P, u=2)
+            for hh in range(2):
+                wt = bank(4 + hh, [P, 2, 2, P], F32, "wt%d" % hh)
+                for jj in range(2):
+                    for u in range(2):
+                        nc.tensor.transpose(wt[:, jj, u, :], w3w[:, 2 * hh + jj, u, :], ident_f[:])
+                src = wt[:].rearrange("p j u c -> p j c u")
+                if hh == 0:
+                    nc.vector.tensor_copy(out=w3gw[:, 0:2], in_=src)
+                else:
+                    nc.scalar.copy(out=w3gw[:, 2:4], in_=src)
+
+        def first_product(t, f):
+            cols = slice(f * P, (f + 1) * P)
+            if f == 0:
+                live["sum"] = bank(7, [P, C], F32, "sum%d" % t)
+            ph = bank(4 + (4 * t + f) % 3, [P, C], F32, "c3_%d_%d" % (t, f))
+            live["ph%d" % f] = ph
+            for dst, first, last in ((ph, True, True), (live["sum"], f == 0, f == 3)):
                 nc.tensor.matmul_mx(
-                    out=u[:], lhsT=eq[:].bitcast(FP8X4), lhsT_scale=es[:],
-                    rhs=c3q[:].bitcast(FP8X4), rhs_scale=c3s[:], start=True, stop=True,
+                    out=dst[:], lhsT=xq[t][:, cols].bitcast(FP8X4), lhsT_scale=xs[t][:, cols],
+                    rhs=w3q[:].bitcast(FP8X4), rhs_scale=w3s[:], start=first, stop=last,
                 )
-                tt = tpool.tile([P, C], F32, tag="tt", name="tt%d" % i)
-                nc.scalar.activation(out=tt[:], in_=u[:], func=ACTF.Copy, scale=rs[:, r:r + 1])
-                v = ps_v.tile([P, 4, P], F32, tag="v", name="v%d" % i)
-                for j in range(4):
-                    nc.tensor.transpose(v[:, j, :], tt[:, j * P:(j + 1) * P], ident_f[:])
-                nc.vector.scalar_tensor_tensor(
-                    out=og[:, :, r * P:(r + 1) * P], in0=v[:], scalar=gam[:, 0:1],
-                    in1=xr[g][:, :, r * P:(r + 1) * P], op0=ALU.mult, op1=ALU.add,
+
+        def pool_start(t):
+            m = mpool.tile([P, C], F32, tag="m", name="m_%d_0" % t)
+            nc.scalar.copy(out=m[:], in_=live["ph0"][:])
+            live["m"] = m
+
+        def pool_max(t, f):
+            m = mpool.tile([P, C], F32, tag="m", name="m_%d_%d" % (t, f))
+            nc.vector.tensor_tensor(out=m[:], in0=live["m"][:], in1=live["ph%d" % f][:], op=ALU.max)
+            live["m"] = m
+
+        def pool_mean(t):
+            smq = mpool.tile([P, C], F32, tag="smq", bufs=2, name="smq%d" % t)
+            nc.scalar.activation(out=smq[:], in_=live["sum"][:], func=ACTF.Copy, scale=0.25)
+            live["smq"] = smq
+
+        def pool_end(t):
+            nc.gpsimd.tensor_tensor(out=c3g[:, :, t], in0=live["m"][:], in1=live["smq"][:], op=ALU.add)
+
+        def scores(i):
+            s = bank(i % 2, [P, M], F32, "s%d" % i)
+            live["s%d" % i] = s
+            for h in range(2):
+                nc.tensor.matmul(
+                    out=s[:], lhsT=c2s[i // 4][:, h, (i % 4) * P:(i % 4 + 1) * P], rhs=c1s[:, h, :],
+                    start=(h == 0), stop=(h == 1),
                 )
-            nc.sync.dma_start(out=out_v[:, :, g * 512:(g + 1) * 512], in_=og[:])
+
+        def row_max(i):
+            nc.vector.tensor_reduce(
+                out=nmx[i // 2][:, i % 2:i % 2 + 1], in_=live["s%d" % i][:], axis=AX.X, op=ALU.max,
+                negate=True,
+            )
+
+        def exponent(i):
+            e = epool.tile([P, M], BF16, tag="e", name="e%d" % i)
+            live["e%d" % i] = e
+            nc.scalar.activation(
+                out=e[:], in_=live["s%d" % i][:], func=ACTF.Exp, bias=nmx[i // 2][:, i % 2:i % 2 + 1],
+                scale=1.0, accum_out=sig[i // 2][:, i % 2:i % 2 + 1],
+            )
+
+        def e_transposes(i):
+            et = bank(2 + i % 2, [P, 4, P], BF16, "et%d" % i)
+            live["et%d" % i] = et
+            for t in range(4):
+                nc.tensor.transpose(et[:, t, :], live["e%d" % i][:, t * P:(t + 1) * P], ident_bf[:])
+
+        def e_regroup(i):
+            nc.scalar.copy(out=eg[i][:], in_=live["et%d" % i][:].rearrange("p t n -> p n t"))
+
+        def e_quantise(i):
+            nc.vector.quantize_mx(
+                out=eq[i][:].bitcast(FP8X4), scales=es[i][:], in_=eg[i][:].rearrange("p n t -> p (n t)")
+            )
+
+        def u_bank(i):
+            return (4, 5)[i % 2] if i < SWITCH else (4, 5, 0, 1)[i % 4]
+
+        def v_bank(i):
+            return (6, 7)[i % 2] if i < SWITCH else (6, 7, 2, 3)[i % 4]
+
+        def second_product(i):
+            u = bank(u_bank(i), [P, C], F32, "u%d" % i)
+            live["u%d" % i] = u
+            nc.tensor.matmul_mx(
+                out=u[:], lhsT=eq[i][:].bitcast(FP8X4), lhsT_scale=es[i][:],
+                rhs=c3q[:].bitcast(FP8X4), rhs_scale=c3s[:], start=True, stop=True,
+            )
+
+        def normalise(i):
+            tt = tpool.tile([P, C], F32, tag="tt", name="tt%d" % i)
+            live["tt%d" % i] = tt
+            nc.scalar.activation(
+                out=tt[:], in_=live["u%d" % i][:], func=ACTF.Copy, scale=rs[i // 2][:, i % 2:i % 2 + 1]
+            )
+
+        def out_transposes(i):
+            v = bank(v_bank(i), [P, 4, P], F32, "v%d" % i)
+            live["v%d" % i] = v
+            for j in range(4):
+                nc.tensor.transpose(v[:, j, :], live["tt%d" % i][:, j * P:(j + 1) * P], ident_f[:])
+
+        def add_x(i):
+            for n, (a, b) in enumerate(STORES):
+                if a <= i < b:
+                    nc.vector.scalar_tensor_tensor(
+                        out=og[n][:, :, (i - a) * P:(i - a + 1) * P], in0=live["v%d" % i][:],
+                        scalar=gam[:, 0:1], in1=xr[i // 4][:, :, (i % 4) * P:(i % 4 + 1) * P],
+                        op0=ALU.mult, op1=ALU.add,
+                    )
+                    if i == b - 1:
+                        nc.sync.dma_start(out=out_v[:, :, a * P:b * P], in_=og[n][:])
+
+        def pair(j):
+            return [i for i in (2 * j, 2 * j + 1) if ok(i)]
+
+        def back_end(j):
+            for i in pair(j - 1):
+                normalise(i)
+            for i in pair(j - 2):
+                add_x(i)
+            for i in pair(j):
+                second_product(i)
+            for i in pair(j - 1):
+                out_transposes(i)
+
+        for t in range(4):
+            regroup_x_on(t, "gpsimd")
+        nc.vector.tensor_copy(out=gam[:], in_=gam_bf[:])
+        for q in range(N_BODIES):
+            a = 2 * q
+            t = q - Q_X
+            has_x = 0 <= t < 4
+            e = q - Q_E
+            if ok(a - 2):
+                exponent(a - 2)
+            if has_x:
+                first_product(t, 0)
+                first_product(t, 1)
+                first_product(t, 2)
+                pool_start(t)
+                first_product(t, 3)
+            if ok(a - 1):
+                exponent(a - 1)
+            if q == 1:
+                w3_transposes()
+            for i in (a, a + 1):
+                if ok(i):
+                    scores(i)
+            if e >= 0:
+                back_end(2 * e)
+            for i in (a - 4, a - 3):
+                if ok(i):
+                    e_regroup(i)
+            for i in (a - 2, a - 1):
+                if ok(i):
+                    e_transposes(i)
+            if has_x:
+                pool_mean(t)
+            for i in (a - 6, a - 5):
+                if ok(i):
+                    e_quantise(i)
+            if ok(a - 4):
+                nc.vector.reciprocal(out=rs[(a - 4) // 2][:], in_=sig[(a - 4) // 2][:])
+            regroup_x_on(t + 1, "vector")
+            if t + 1 == 0:
+                nc.vector.quantize_mx(out=w3q[:].bitcast(FP8X4), scales=w3s[:], in_=w3g[:])
+            if 0 <= t + 1 < 4:
+                quantise_x(t + 1)
+            if has_x:
+                pool_max(t, 1)
+                pool_max(t, 2)
+                pool_max(t, 3)
+                pool_end(t)
+            if t == 4:
+                nc.vector.quantize_mx(
+                    out=c3q[:].bitcast(FP8X4), scales=c3s[:], in_=c3g[:].rearrange("p c t -> p (c t)")
+                )
+            if e >= 0:
+                back_end(2 * e + 1)
+            for i in (a, a + 1):
+                if ok(i):
+                    row_max(i)

@@ -19,10 +19,6 @@ NPIX = 2048
 NT = NPIX // P
 FLOPS = 2 * (C * C * NPIX + NPIX * M * 256 + C * M * NPIX)
 
-Q_X = 2
-Q_E = 7
-N_BODIES = 12
-SWITCH = 8
 STORES = ((0, 4), (4, 8), (8, 12), (12, 14), (14, 16))
 
 
@@ -36,7 +32,6 @@ def tile_selfspatialattentionmodule_pb_kernel(tc, x, c2, c1p, W3, gamma, out):
 
     with ExitStack() as ctx:
         keep = ctx.enter_context(tc.tile_pool(name="keep", bufs=1))
-        epool = ctx.enter_context(tc.tile_pool(name="epool", bufs=4))
         mpool = ctx.enter_context(tc.tile_pool(name="mpool", bufs=6))
         tpool = ctx.enter_context(tc.tile_pool(name="tpool", bufs=4))
         psum = ctx.enter_context(tc.psum_pool(name="psum", bufs=1))
@@ -51,22 +46,13 @@ def tile_selfspatialattentionmodule_pb_kernel(tc, x, c2, c1p, W3, gamma, out):
         w3r = keep.tile([P, 4 * C], BF16, name="w3r")
         gam_bf = keep.tile([P, 1], BF16, name="gam_bf")
 
-        def load_c2(g):
-            nc.sync.dma_start(out=c2s[g][:], in_=c2_v[:, :, g * 512:(g + 1) * 512])
-
-        def load_x(g):
-            nc.sync.dma_start(out=xr[g][:], in_=x_v[:, :, g * 512:(g + 1) * 512])
-
         nc.sync.dma_start(out=c1s[:], in_=c1_v)
-        load_c2(0)
+        nc.sync.dma_start(out=c2s[0][:], in_=c2_v[:, :, 0:512])
         nc.sync.dma_start(out=w3r[:], in_=w3_v)
-        load_x(0)
-        load_x(1)
-        load_c2(1)
-        load_x(2)
-        load_x(3)
-        load_c2(2)
-        load_c2(3)
+        for g in range(1, 4):
+            nc.sync.dma_start(out=c2s[g][:], in_=c2_v[:, :, g * 512:(g + 1) * 512])
+        for g in range(4):
+            nc.sync.dma_start(out=xr[g][:], in_=x_v[:, :, g * 512:(g + 1) * 512])
         nc.scalar.dma_start(out=gam_bf[:], in_=gamma.partition_broadcast(P))
 
         warm = keep.tile([P, 1], F32, name="warm")
@@ -77,6 +63,7 @@ def tile_selfspatialattentionmodule_pb_kernel(tc, x, c2, c1p, W3, gamma, out):
         ident_bf = keep.tile([P, P], BF16, name="ident_bf")
         make_identity(nc, ident_bf[:])
         gam = keep.tile([P, 1], F32, name="gam")
+        nc.vector.tensor_copy(out=gam[:], in_=gam_bf[:])
 
         w3g = keep.tile([P, 4 * C], BF16, name="w3g", align_bytes=64)
         w3q = keep.tile([P, C], U32, name="w3q", align_bytes=64)
@@ -87,37 +74,23 @@ def tile_selfspatialattentionmodule_pb_kernel(tc, x, c2, c1p, W3, gamma, out):
         c3g = keep.tile([P, C, 4], BF16, name="c3g", align_bytes=64)
         c3q = keep.tile([P, C], U32, name="c3q", align_bytes=64)
         c3s = keep.tile([P, C], U8, name="c3s", align_bytes=64)
+        ee = [keep.tile([P, M], BF16, name="ee%d" % i) for i in range(NT)]
         eg = [keep.tile([P, P, 4], BF16, name="eg%d" % i, align_bytes=64) for i in range(NT)]
         eq = [keep.tile([P, P], U32, name="eq%d" % i, align_bytes=64) for i in range(NT)]
         es = [keep.tile([P, P], U8, name="es%d" % i, align_bytes=64) for i in range(NT)]
-        nmx = [keep.tile([P, 2], F32, name="nmx%d" % i) for i in range(NT // 2)]
-        sig = [keep.tile([P, 2], F32, name="sig%d" % i) for i in range(NT // 2)]
-        rs = [keep.tile([P, 2], F32, name="rs%d" % i) for i in range(NT // 2)]
+        nmx = keep.tile([P, NT], F32, name="nmx")
+        sig = keep.tile([P, NT], F32, name="sig")
+        rs = keep.tile([P, NT], F32, name="rs")
         og = [keep.tile([P, 4, (b - a) * P], F32, name="og%d" % a) for (a, b) in STORES]
         live = {}
 
-        def ok(i):
-            return 0 <= i < NT
-
-        def regroup_x(t, f, eng):
+        def regroup_x(t, f):
             src = xr[t][:].rearrange("p j (a dh jj dw) -> p dh dw a jj j", a=8, dh=2, jj=16, dw=2)
             dst = xg[t][:, f].rearrange("p (a jj) j -> p a jj j", a=8)
-            if eng == "vector":
-                nc.vector.tensor_copy(out=dst, in_=src[:, f // 2, f % 2])
-            else:
-                nc.gpsimd.tensor_scalar(
-                    out=dst, in0=src[:, f // 2, f % 2], scalar1=1.0, scalar2=0.0,
-                    op0=ALU.mult, op1=ALU.add,
-                )
-
-        def x_engine(t, f):
-            return "vector" if (t == 0 or f == 0) else "gpsimd"
-
-        def regroup_x_on(t, eng):
-            if 0 <= t < 4:
-                for f in range(4):
-                    if x_engine(t, f) == eng:
-                        regroup_x(t, f, eng)
+            nc.gpsimd.tensor_scalar(
+                out=dst, in0=src[:, f // 2, f % 2], scalar1=1.0, scalar2=0.0,
+                op0=ALU.mult, op1=ALU.add,
+            )
 
         def quantise_x(t):
             nc.vector.quantize_mx(
@@ -127,29 +100,24 @@ def tile_selfspatialattentionmodule_pb_kernel(tc, x, c2, c1p, W3, gamma, out):
 
         def w3_transposes():
             w3w = w3r[:].bitcast(F32).rearrange("p (j w u) -> p j u w", j=4, w=P, u=2)
-            w3gw = w3g[:].bitcast(F32).rearrange("p (j c u) -> p j c u", j=4, c=P, u=2)
             for hh in range(2):
-                wt = bank(4 + hh, [P, 2, 2, P], F32, "wt%d" % hh)
+                wt = bank(6 + hh, [P, 2, 2, P], F32, "wt%d" % hh)
+                live["wt%d" % hh] = wt
                 for jj in range(2):
                     for u in range(2):
                         nc.tensor.transpose(wt[:, jj, u, :], w3w[:, 2 * hh + jj, u, :], ident_f[:])
-                src = wt[:].rearrange("p j u c -> p j c u")
-                if hh == 0:
-                    nc.vector.tensor_copy(out=w3gw[:, 0:2], in_=src)
-                else:
-                    nc.scalar.copy(out=w3gw[:, 2:4], in_=src)
 
-        def first_product(t, f):
+        def w3_regroup():
+            w3gw = w3g[:].bitcast(F32).rearrange("p (j c u) -> p j c u", j=4, c=P, u=2)
+            nc.vector.tensor_copy(out=w3gw[:, 0:2], in_=live["wt0"][:].rearrange("p j u c -> p j c u"))
+            nc.scalar.copy(out=w3gw[:, 2:4], in_=live["wt1"][:].rearrange("p j u c -> p j c u"))
+
+        def mx_first(dst, t, f, first, last):
             cols = slice(f * P, (f + 1) * P)
-            if f == 0:
-                live["sum"] = bank(7, [P, C], F32, "sum%d" % t)
-            ph = bank(4 + (4 * t + f) % 3, [P, C], F32, "c3_%d_%d" % (t, f))
-            live["ph%d" % f] = ph
-            for dst, first, last in ((ph, True, True), (live["sum"], f == 0, f == 3)):
-                nc.tensor.matmul_mx(
-                    out=dst[:], lhsT=xq[t][:, cols].bitcast(FP8X4), lhsT_scale=xs[t][:, cols],
-                    rhs=w3q[:].bitcast(FP8X4), rhs_scale=w3s[:], start=first, stop=last,
-                )
+            nc.tensor.matmul_mx(
+                out=dst[:], lhsT=xq[t][:, cols].bitcast(FP8X4), lhsT_scale=xs[t][:, cols],
+                rhs=w3q[:].bitcast(FP8X4), rhs_scale=w3s[:], start=first, stop=last,
+            )
 
         def pool_start(t):
             m = mpool.tile([P, C], F32, tag="m", name="m_%d_0" % t)
@@ -170,7 +138,7 @@ def tile_selfspatialattentionmodule_pb_kernel(tc, x, c2, c1p, W3, gamma, out):
             nc.gpsimd.tensor_tensor(out=c3g[:, :, t], in0=live["m"][:], in1=live["smq"][:], op=ALU.add)
 
         def scores(i):
-            s = bank(i % 2, [P, M], F32, "s%d" % i)
+            s = bank(i % 6, [P, M], F32, "s%d" % i)
             live["s%d" % i] = s
             for h in range(2):
                 nc.tensor.matmul(
@@ -180,40 +148,35 @@ def tile_selfspatialattentionmodule_pb_kernel(tc, x, c2, c1p, W3, gamma, out):
 
         def row_max(i):
             nc.vector.tensor_reduce(
-                out=nmx[i // 2][:, i % 2:i % 2 + 1], in_=live["s%d" % i][:], axis=AX.X, op=ALU.max,
-                negate=True,
+                out=nmx[:, i:i + 1], in_=live["s%d" % i][:], axis=AX.X, op=ALU.max, negate=True
             )
 
         def exponent(i):
-            e = epool.tile([P, M], BF16, tag="e", name="e%d" % i)
-            live["e%d" % i] = e
             nc.scalar.activation(
-                out=e[:], in_=live["s%d" % i][:], func=ACTF.Exp, bias=nmx[i // 2][:, i % 2:i % 2 + 1],
-                scale=1.0, accum_out=sig[i // 2][:, i % 2:i % 2 + 1],
+                out=ee[i][:], in_=live["s%d" % i][:], func=ACTF.Exp, bias=nmx[:, i:i + 1],
+                scale=1.0, accum_out=sig[:, i:i + 1],
             )
 
-        def e_transposes(i):
-            et = bank(2 + i % 2, [P, 4, P], BF16, "et%d" % i)
+        def e_transposes(i, n):
+            et = bank(n, [P, 4, P], BF16, "et%d" % i)
             live["et%d" % i] = et
             for t in range(4):
-                nc.tensor.transpose(et[:, t, :], live["e%d" % i][:, t * P:(t + 1) * P], ident_bf[:])
+                nc.tensor.transpose(et[:, t, :], ee[i][:, t * P:(t + 1) * P], ident_bf[:])
 
-        def e_regroup(i):
-            nc.scalar.copy(out=eg[i][:], in_=live["et%d" % i][:].rearrange("p t n -> p n t"))
+        def e_regroup(i, eng):
+            src = live["et%d" % i][:].rearrange("p t n -> p n t")
+            if eng == "scalar":
+                nc.scalar.copy(out=eg[i][:], in_=src)
+            else:
+                nc.vector.tensor_copy(out=eg[i][:], in_=src)
 
         def e_quantise(i):
             nc.vector.quantize_mx(
                 out=eq[i][:].bitcast(FP8X4), scales=es[i][:], in_=eg[i][:].rearrange("p n t -> p (n t)")
             )
 
-        def u_bank(i):
-            return (4, 5)[i % 2] if i < SWITCH else (4, 5, 0, 1)[i % 4]
-
-        def v_bank(i):
-            return (6, 7)[i % 2] if i < SWITCH else (6, 7, 2, 3)[i % 4]
-
         def second_product(i):
-            u = bank(u_bank(i), [P, C], F32, "u%d" % i)
+            u = bank(i % 4, [P, C], F32, "u%d" % i)
             live["u%d" % i] = u
             nc.tensor.matmul_mx(
                 out=u[:], lhsT=eq[i][:].bitcast(FP8X4), lhsT_scale=es[i][:],
@@ -223,12 +186,10 @@ def tile_selfspatialattentionmodule_pb_kernel(tc, x, c2, c1p, W3, gamma, out):
         def normalise(i):
             tt = tpool.tile([P, C], F32, tag="tt", name="tt%d" % i)
             live["tt%d" % i] = tt
-            nc.scalar.activation(
-                out=tt[:], in_=live["u%d" % i][:], func=ACTF.Copy, scale=rs[i // 2][:, i % 2:i % 2 + 1]
-            )
+            nc.scalar.activation(out=tt[:], in_=live["u%d" % i][:], func=ACTF.Copy, scale=rs[:, i:i + 1])
 
         def out_transposes(i):
-            v = bank(v_bank(i), [P, 4, P], F32, "v%d" % i)
+            v = bank(4 + i % 4, [P, 4, P], F32, "v%d" % i)
             live["v%d" % i] = v
             for j in range(4):
                 nc.tensor.transpose(v[:, j, :], live["tt%d" % i][:, j * P:(j + 1) * P], ident_f[:])
@@ -245,72 +206,70 @@ def tile_selfspatialattentionmodule_pb_kernel(tc, x, c2, c1p, W3, gamma, out):
                         nc.sync.dma_start(out=out_v[:, :, a * P:b * P], in_=og[n][:])
 
         def pair(j):
-            return [i for i in (2 * j, 2 * j + 1) if ok(i)]
-
-        def back_end(j):
-            for i in pair(j - 1):
-                normalise(i)
-            for i in pair(j - 2):
-                add_x(i)
-            for i in pair(j):
-                second_product(i)
-            for i in pair(j - 1):
-                out_transposes(i)
+            return [i for i in (2 * j, 2 * j + 1) if 0 <= i < NT]
 
         for t in range(4):
-            regroup_x_on(t, "gpsimd")
-        nc.vector.tensor_copy(out=gam[:], in_=gam_bf[:])
-        for q in range(N_BODIES):
-            a = 2 * q
-            t = q - Q_X
-            has_x = 0 <= t < 4
-            e = q - Q_E
-            if ok(a - 2):
-                exponent(a - 2)
-            if has_x:
-                first_product(t, 0)
-                first_product(t, 1)
-                first_product(t, 2)
-                pool_start(t)
-                first_product(t, 3)
-            if ok(a - 1):
-                exponent(a - 1)
-            if q == 1:
+            for f in range(4):
+                regroup_x(t, f)
+
+        for i in range(NT):
+            scores(i)
+            if i == 3:
                 w3_transposes()
-            for i in (a, a + 1):
-                if ok(i):
-                    scores(i)
-            if e >= 0:
-                back_end(2 * e)
-            for i in (a - 4, a - 3):
-                if ok(i):
-                    e_regroup(i)
-            for i in (a - 2, a - 1):
-                if ok(i):
-                    e_transposes(i)
-            if has_x:
-                pool_mean(t)
-            for i in (a - 6, a - 5):
-                if ok(i):
-                    e_quantise(i)
-            if ok(a - 4):
-                nc.vector.reciprocal(out=rs[(a - 4) // 2][:], in_=sig[(a - 4) // 2][:])
-            regroup_x_on(t + 1, "vector")
-            if t + 1 == 0:
+            row_max(i)
+            exponent(i)
+            if i == 6:
+                w3_regroup()
+            if i == 9:
                 nc.vector.quantize_mx(out=w3q[:].bitcast(FP8X4), scales=w3s[:], in_=w3g[:])
-            if 0 <= t + 1 < 4:
-                quantise_x(t + 1)
-            if has_x:
-                pool_max(t, 1)
-                pool_max(t, 2)
-                pool_max(t, 3)
-                pool_end(t)
-            if t == 4:
+            if i == 12:
+                quantise_x(0)
+            if i == 15:
+                quantise_x(1)
+
+        for t in range(4):
+            for f in range(4):
+                live["ph%d" % f] = bank((6, 7, 4, 5)[f], [P, C], F32, "c3_%d_%d" % (t, f))
+                mx_first(live["ph%d" % f], t, f, True, True)
+            if t + 2 < 4:
+                quantise_x(t + 2)
+            pool_start(t)
+            live["sum"] = bank(t % 2, [P, C], F32, "sum%d" % t)
+            for f in range(4):
+                mx_first(live["sum"], t, f, f == 0, f == 3)
+            for i in pair(t - 2):
+                e_quantise(i)
+            pool_max(t, 1)
+            for i in pair(t - 1):
+                e_regroup(i, "scalar")
+            for i in pair(t):
+                e_transposes(i, 2 + i % 2)
+            pool_mean(t)
+            pool_max(t, 2)
+            pool_max(t, 3)
+            pool_end(t)
+
+        nc.vector.reciprocal(out=rs[:], in_=sig[:])
+        for i in range(8, NT + 2):
+            if i < NT:
+                e_transposes(i, (2, 3, 6, 7, 4, 5)[i % 6])
+            e_regroup(i - 2, "scalar" if i % 2 == 0 else "vector")
+            if i < NT:
+                e_quantise(i - 4)
+            if i == 12:
                 nc.vector.quantize_mx(
                     out=c3q[:].bitcast(FP8X4), scales=c3s[:], in_=c3g[:].rearrange("p c t -> p (c t)")
                 )
-            if e >= 0:
-                back_end(2 * e + 1)
-            for i in (a, a + 1):
-                if ok(i):
-                    row_max(i)
+
+        for e in range(NT // 2 + 3):
+            for i in pair(e + 1):
+                if i >= 12:
+                    e_quantise(i)
+            for i in pair(e - 1):
+                normalise(i)
+            for i in pair(e - 2):
+                out_transposes(i)
+            for i in pair(e):
+                second_product(i)
+            for i in pair(e - 3):
+                add_x(i)

@@ -17,28 +17,37 @@ C = 512
 M = 512
 NPIX = 2048
 NT = NPIX // P
+NPAIR = NT // 2
+WARM = 4
+VECTOR_ADDS = ((1, 3),)
+WIDE = 2
 FLOPS = 2 * (C * C * NPIX + NPIX * M * 256 + C * M * NPIX)
-
-STORES = ((0, 4), (4, 8), (8, 12), (12, 14), (14, 16))
 
 
 def tile_selfspatialattentionmodule_pb_kernel(tc, x, c2, c1p, W3, gamma, out):
     nc = tc.nc
     x_v = x[0].rearrange("(p j) h w -> p j (h w)", j=4)
     out_v = out[0].rearrange("(p j) h w -> p j (h w)", j=4)
-    c2_v = c2[0].rearrange("(g p) h w -> p g (h w)", p=P)
-    c1_v = c1p[0].rearrange("(g p) h w -> p g (h w)", p=P)
+    c2_v = c2[0].rearrange("(p g) h w -> p g (h w)", g=2)
+    c1_v = c1p[0].rearrange("(p g) h w -> p g (h w)", g=2)
     w3_v = W3.rearrange("(p j) k -> p (j k)", j=4)
 
     with ExitStack() as ctx:
         keep = ctx.enter_context(tc.tile_pool(name="keep", bufs=1))
-        mpool = ctx.enter_context(tc.tile_pool(name="mpool", bufs=6))
-        tpool = ctx.enter_context(tc.tile_pool(name="tpool", bufs=4))
+        work = ctx.enter_context(tc.tile_pool(name="work", bufs=4))
         psum = ctx.enter_context(tc.psum_pool(name="psum", bufs=1))
         ctx.enter_context(tc.manual_schedule())
+        live = {}
+        free = list(range(8))
+        held = {}
 
-        def bank(n, shape, dtype, name):
-            return psum.tile(shape, dtype, tag="bank%d" % n, name=name)
+        def take(name, shape, dtype):
+            held[name] = free.pop(0)
+            live[name] = psum.tile(shape, dtype, tag="bank%d" % held[name], name=name)
+            return live[name]
+
+        def give(name):
+            free.append(held[name])
 
         c1s = keep.tile([P, 2, M], BF16, name="c1s")
         c2s = [keep.tile([P, 2, 512], BF16, name="c2s%d" % g) for g in range(4)]
@@ -46,24 +55,36 @@ def tile_selfspatialattentionmodule_pb_kernel(tc, x, c2, c1p, W3, gamma, out):
         w3r = keep.tile([P, 4 * C], BF16, name="w3r")
         gam_bf = keep.tile([P, 1], BF16, name="gam_bf")
 
-        nc.sync.dma_start(out=c1s[:], in_=c1_v)
-        nc.sync.dma_start(out=c2s[0][:], in_=c2_v[:, :, 0:512])
-        nc.sync.dma_start(out=w3r[:], in_=w3_v)
-        for g in range(1, 4):
+        def load_c2(g):
             nc.sync.dma_start(out=c2s[g][:], in_=c2_v[:, :, g * 512:(g + 1) * 512])
-        for g in range(4):
+
+        def load_x(g):
             nc.sync.dma_start(out=xr[g][:], in_=x_v[:, :, g * 512:(g + 1) * 512])
+
+        for h in range(2):
+            nc.sync.dma_start(out=c1s[:, h, :], in_=c1_v[:, h, :])
+            nc.sync.dma_start(out=c2s[0][:, h, :], in_=c2_v[:, h, 0:512])
+        load_x(0)
+        load_c2(1)
+        nc.sync.dma_start(out=w3r[:], in_=w3_v)
+        load_c2(2)
+        load_x(1)
+        load_c2(3)
+        load_x(2)
+        load_x(3)
         nc.scalar.dma_start(out=gam_bf[:], in_=gamma.partition_broadcast(P))
 
         warm = keep.tile([P, 1], F32, name="warm")
         nc.vector.memset(warm[:], 0.0)
         nc.scalar.activation(out=warm[:], in_=warm[:], func=ACTF.Exp)
+        idle = keep.tile([P, 512], BF16, name="idle")
+        nc.vector.memset(idle[:], 0.0)
+        wb = psum.tile([P, 512], F32, tag="bank7", name="wb")
+        for n in range(WARM):
+            nc.tensor.matmul(out=wb[:], lhsT=idle[:, 0:P], rhs=idle[:], start=True, stop=True)
         ident_f = keep.tile([P, P], F32, name="ident_f")
         make_identity(nc, ident_f[:])
-        ident_bf = keep.tile([P, P], BF16, name="ident_bf")
-        make_identity(nc, ident_bf[:])
         gam = keep.tile([P, 1], F32, name="gam")
-        nc.vector.tensor_copy(out=gam[:], in_=gam_bf[:])
 
         w3g = keep.tile([P, 4 * C], BF16, name="w3g", align_bytes=64)
         w3q = keep.tile([P, C], U32, name="w3q", align_bytes=64)
@@ -71,46 +92,47 @@ def tile_selfspatialattentionmodule_pb_kernel(tc, x, c2, c1p, W3, gamma, out):
         xg = [keep.tile([P, 4, P, 4], BF16, name="xg%d" % t, align_bytes=64) for t in range(4)]
         xq = [keep.tile([P, 4 * P], U32, name="xq%d" % t, align_bytes=64) for t in range(4)]
         xs = [keep.tile([P, 4 * P], U8, name="xs%d" % t, align_bytes=64) for t in range(4)]
-        c3g = keep.tile([P, C, 4], BF16, name="c3g", align_bytes=64)
+        c3w = keep.tile([P, 4, C], BF16, name="c3w")
+        c3g = [keep.tile([P, P, 4], BF16, name="c3g%d" % j, align_bytes=64) for j in range(4)]
         c3q = keep.tile([P, C], U32, name="c3q", align_bytes=64)
         c3s = keep.tile([P, C], U8, name="c3s", align_bytes=64)
-        ee = [keep.tile([P, M], BF16, name="ee%d" % i) for i in range(NT)]
-        eg = [keep.tile([P, P, 4], BF16, name="eg%d" % i, align_bytes=64) for i in range(NT)]
-        eq = [keep.tile([P, P], U32, name="eq%d" % i, align_bytes=64) for i in range(NT)]
-        es = [keep.tile([P, P], U8, name="es%d" % i, align_bytes=64) for i in range(NT)]
+        eg = [keep.tile([P, 2, P, 4], BF16, name="eg%d" % k, align_bytes=64) for k in range(NPAIR)]
+        eq = [keep.tile([P, 512], U32, name="eq%d" % g, align_bytes=64) for g in range(4)]
+        es = [keep.tile([P, 512], U8, name="es%d" % g, align_bytes=64) for g in range(4)]
         nmx = keep.tile([P, NT], F32, name="nmx")
         sig = keep.tile([P, NT], F32, name="sig")
+        ri = keep.tile([P, NT], F32, name="ri")
         rs = keep.tile([P, NT], F32, name="rs")
-        og = [keep.tile([P, 4, (b - a) * P], F32, name="og%d" % a) for (a, b) in STORES]
-        live = {}
+        rsb = keep.tile([P, WIDE, 512], F32, name="rsb")
 
         def regroup_x(t, f):
             src = xr[t][:].rearrange("p j (a dh jj dw) -> p dh dw a jj j", a=8, dh=2, jj=16, dw=2)
             dst = xg[t][:, f].rearrange("p (a jj) j -> p a jj j", a=8)
             nc.gpsimd.tensor_scalar(
-                out=dst, in0=src[:, f // 2, f % 2], scalar1=1.0, scalar2=0.0,
-                op0=ALU.mult, op1=ALU.add,
+                out=dst, in0=src[:, f // 2, f % 2], scalar1=1.0, scalar2=0.0, op0=ALU.mult, op1=ALU.add
             )
 
         def quantise_x(t):
             nc.vector.quantize_mx(
-                out=xq[t][:].bitcast(FP8X4), scales=xs[t][:],
-                in_=xg[t][:].rearrange("p f c j -> p (f c j)"),
+                out=xq[t][:].bitcast(FP8X4), scales=xs[t][:], in_=xg[t][:].rearrange("p f c j -> p (f c j)")
             )
 
-        def w3_transposes():
+        def w3_transposes(half):
             w3w = w3r[:].bitcast(F32).rearrange("p (j w u) -> p j u w", j=4, w=P, u=2)
-            for hh in range(2):
-                wt = bank(6 + hh, [P, 2, 2, P], F32, "wt%d" % hh)
-                live["wt%d" % hh] = wt
-                for jj in range(2):
-                    for u in range(2):
-                        nc.tensor.transpose(wt[:, jj, u, :], w3w[:, 2 * hh + jj, u, :], ident_f[:])
+            wt = take("wt%d" % half, [P, 2, 2, P], F32)
+            for jj in range(2):
+                for u in range(2):
+                    nc.tensor.transpose(wt[:, jj, u, :], w3w[:, 2 * half + jj, u, :], ident_f[:])
 
-        def w3_regroup():
+        def w3_regroup(half):
             w3gw = w3g[:].bitcast(F32).rearrange("p (j c u) -> p j c u", j=4, c=P, u=2)
-            nc.vector.tensor_copy(out=w3gw[:, 0:2], in_=live["wt0"][:].rearrange("p j u c -> p j c u"))
-            nc.scalar.copy(out=w3gw[:, 2:4], in_=live["wt1"][:].rearrange("p j u c -> p j c u"))
+            nc.scalar.copy(
+                out=w3gw[:, 2 * half:2 * half + 2], in_=live["wt%d" % half][:].rearrange("p j u c -> p j c u")
+            )
+            give("wt%d" % half)
+
+        def w3_quantise():
+            nc.vector.quantize_mx(out=w3q[:].bitcast(FP8X4), scales=w3s[:], in_=w3g[:])
 
         def mx_first(dst, t, f, first, last):
             cols = slice(f * P, (f + 1) * P)
@@ -119,27 +141,60 @@ def tile_selfspatialattentionmodule_pb_kernel(tc, x, c2, c1p, W3, gamma, out):
                 rhs=w3q[:].bitcast(FP8X4), rhs_scale=w3s[:], start=first, stop=last,
             )
 
+        def pixel_product(t, f):
+            mx_first(take("ph%d%d" % (t, f), [P, C], F32), t, f, True, True)
+
+        def sum_product(t):
+            total = take("sum%d" % t, [P, C], F32)
+            for f in range(4):
+                mx_first(total, t, f, f == 0, f == 3)
+
         def pool_start(t):
-            m = mpool.tile([P, C], F32, tag="m", name="m_%d_0" % t)
-            nc.scalar.copy(out=m[:], in_=live["ph0"][:])
-            live["m"] = m
+            m = work.tile([P, C], F32, tag="m", bufs=8, name="m_%d_0" % t)
+            nc.scalar.copy(out=m[:], in_=live["ph%d0" % t][:])
+            give("ph%d0" % t)
+            live["m%d" % t] = m
 
         def pool_max(t, f):
-            m = mpool.tile([P, C], F32, tag="m", name="m_%d_%d" % (t, f))
-            nc.vector.tensor_tensor(out=m[:], in0=live["m"][:], in1=live["ph%d" % f][:], op=ALU.max)
-            live["m"] = m
+            m = work.tile([P, C], F32, tag="m", bufs=8, name="m_%d_%d" % (t, f))
+            nc.vector.tensor_tensor(out=m[:], in0=live["m%d" % t][:], in1=live["ph%d%d" % (t, f)][:], op=ALU.max)
+            live["m%d" % t] = m
+            give("ph%d%d" % (t, f))
 
         def pool_mean(t):
-            smq = mpool.tile([P, C], F32, tag="smq", bufs=2, name="smq%d" % t)
-            nc.scalar.activation(out=smq[:], in_=live["sum"][:], func=ACTF.Copy, scale=0.25)
-            live["smq"] = smq
+            smq = work.tile([P, C], F32, tag="smq", name="smq%d" % t)
+            nc.scalar.activation(out=smq[:], in_=live["sum%d" % t][:], func=ACTF.Copy, scale=0.25)
+            live["smq%d" % t] = smq
+            give("sum%d" % t)
 
         def pool_end(t):
-            nc.gpsimd.tensor_tensor(out=c3g[:, :, t], in0=live["m"][:], in1=live["smq"][:], op=ALU.add)
+            nc.gpsimd.tensor_tensor(out=c3w[:, t, :], in0=live["m%d" % t][:], in1=live["smq%d" % t][:], op=ALU.add)
+
+        def pool_end_last(t, half):
+            cols = slice(half * 256, (half + 1) * 256)
+            nc.vector.scalar_tensor_tensor(
+                out=c3w[:, t, cols], in0=live["sum%d" % t][:, cols], scalar=0.25, in1=live["m%d" % t][:, cols],
+                op0=ALU.mult, op1=ALU.add,
+            )
+            if half == 1:
+                give("sum%d" % t)
+
+        def c3_interleave(j, eng):
+            src = c3w[:, :, j * P:(j + 1) * P].rearrange("p t c -> p c t")
+            if eng == "scalar":
+                nc.scalar.copy(out=c3g[j][:], in_=src)
+            elif eng == "gpsimd":
+                nc.gpsimd.tensor_scalar(out=c3g[j][:], in0=src, scalar1=1.0, scalar2=0.0, op0=ALU.mult, op1=ALU.add)
+            else:
+                nc.vector.tensor_copy(out=c3g[j][:], in_=src)
+
+        def c3_quantise(j):
+            nc.vector.quantize_mx(
+                out=c3q[:, j * P:(j + 1) * P].bitcast(FP8X4), scales=c3s[:, j * P:(j + 1) * P], in_=c3g[j][:].rearrange("p c t -> p (c t)")
+            )
 
         def scores(i):
-            s = bank(i % 6, [P, M], F32, "s%d" % i)
-            live["s%d" % i] = s
+            s = take("s%d" % i, [P, M], F32)
             for h in range(2):
                 nc.tensor.matmul(
                     out=s[:], lhsT=c2s[i // 4][:, h, (i % 4) * P:(i % 4 + 1) * P], rhs=c1s[:, h, :],
@@ -152,124 +207,228 @@ def tile_selfspatialattentionmodule_pb_kernel(tc, x, c2, c1p, W3, gamma, out):
             )
 
         def exponent(i):
+            ee = keep.tile([P, M], BF16, name="ee%d" % i)
+            live["ee%d" % i] = ee
             nc.scalar.activation(
-                out=ee[i][:], in_=live["s%d" % i][:], func=ACTF.Exp, bias=nmx[:, i:i + 1],
-                scale=1.0, accum_out=sig[:, i:i + 1],
+                out=ee[:].rearrange("p (u q e) -> p u q e", u=2, e=2),
+                in_=live["s%d" % i][:].rearrange("p (u e q) -> p u q e", u=2, e=2),
+                func=ACTF.Exp, bias=nmx[:, i:i + 1], scale=1.0, accum_out=sig[:, i:i + 1],
             )
+            give("s%d" % i)
 
-        def e_transposes(i, n):
-            et = bank(n, [P, 4, P], BF16, "et%d" % i)
-            live["et%d" % i] = et
-            for t in range(4):
-                nc.tensor.transpose(et[:, t, :], ee[i][:, t * P:(t + 1) * P], ident_bf[:])
+        def e_transposes(k):
+            et = take("et%d" % k, [P, 2, 2, P], F32)
+            for i in range(2):
+                words = live["ee%d" % (2 * k + i)][:].bitcast(F32)
+                for u in range(2):
+                    nc.tensor.transpose(et[:, i, u, :], words[:, u * P:(u + 1) * P], ident_f[:])
 
-        def e_regroup(i, eng):
-            src = live["et%d" % i][:].rearrange("p t n -> p n t")
-            if eng == "scalar":
-                nc.scalar.copy(out=eg[i][:], in_=src)
-            else:
-                nc.vector.tensor_copy(out=eg[i][:], in_=src)
+        def e_regroup(k):
+            dst = eg[k][:].rearrange("p i n t -> p (i n t)").bitcast(F32)
+            nc.scalar.copy(
+                out=dst.rearrange("p (i n u) -> p i n u", i=2, u=2),
+                in_=live["et%d" % k][:].rearrange("p i u n -> p i n u"),
+            )
+            give("et%d" % k)
 
-        def e_quantise(i):
+        def e_quantise(k):
+            cols = slice((k % 2) * 2 * P, (k % 2 + 1) * 2 * P)
             nc.vector.quantize_mx(
-                out=eq[i][:].bitcast(FP8X4), scales=es[i][:], in_=eg[i][:].rearrange("p n t -> p (n t)")
+                out=eq[k // 2][:, cols].bitcast(FP8X4), scales=es[k // 2][:, cols],
+                in_=eg[k][:].rearrange("p i n t -> p (i n t)"),
             )
 
-        def second_product(i):
-            u = bank(i % 4, [P, C], F32, "u%d" % i)
-            live["u%d" % i] = u
+        def norm():
+            nc.vector.reciprocal(out=ri[:], in_=sig[:])
+            nc.gpsimd.tensor_scalar(out=rs[:], in0=ri[:], scalar1=gam[:, 0:1], scalar2=0.0, op0=ALU.mult, op1=ALU.add)
+
+        def norm_transposes(g):
+            r = take("rb%d" % g, [P, 4, P], F32)
+            for i in range(4):
+                col = rs[:, 4 * g + i:4 * g + i + 1]
+                nc.tensor.transpose(r[:, i, :], col.to_broadcast([P, P]), ident_f[:])
+
+        def norm_copy(g):
+            nc.scalar.copy(out=rsb[:, g, :], in_=live["rb%d" % g][:].rearrange("p i n -> p (i n)"))
+            give("rb%d" % g)
+
+        def wide_product(g, j):
+            u = take("w%d_%d" % (g, j), [P, 512], F32)
             nc.tensor.matmul_mx(
-                out=u[:], lhsT=eq[i][:].bitcast(FP8X4), lhsT_scale=es[i][:],
+                out=u[:], lhsT=c3q[:, j * P:(j + 1) * P].bitcast(FP8X4), lhsT_scale=c3s[:, j * P:(j + 1) * P],
+                rhs=eq[g][:].bitcast(FP8X4), rhs_scale=es[g][:], start=True, stop=True,
+            )
+
+        def wide_normalise(g, j):
+            tt = work.tile([P, 512], F32, tag="tw", name="tw%d_%d" % (g, j))
+            live["tw%d_%d" % (g, j)] = tt
+            nc.vector.tensor_tensor(out=tt[:], in0=live["w%d_%d" % (g, j)][:], in1=rsb[:, g, :], op=ALU.mult)
+            give("w%d_%d" % (g, j))
+
+        def wide_add(g, j):
+            o = work.tile([P, 512], F32, tag="ow", bufs=8, name="ow%d_%d" % (g, j))
+            live["ow%d_%d" % (g, j)] = o
+            eng = nc.vector if (g, j) in VECTOR_ADDS else nc.gpsimd
+            eng.tensor_tensor(out=o[:], in0=live["tw%d_%d" % (g, j)][:], in1=xr[g][:, j, :], op=ALU.add)
+
+        def wide_store(g, j):
+            nc.sync.dma_start(out=out_v[:, j, g * 512:(g + 1) * 512], in_=live["ow%d_%d" % (g, j)][:])
+
+        def tall_product(i):
+            u = take("u%d" % i, [P, C], F32)
+            cols = slice((i % 4) * P, (i % 4 + 1) * P)
+            nc.tensor.matmul_mx(
+                out=u[:], lhsT=eq[i // 4][:, cols].bitcast(FP8X4), lhsT_scale=es[i // 4][:, cols],
                 rhs=c3q[:].bitcast(FP8X4), rhs_scale=c3s[:], start=True, stop=True,
             )
 
-        def normalise(i):
-            tt = tpool.tile([P, C], F32, tag="tt", name="tt%d" % i)
+        def tall_normalise(i):
+            tt = work.tile([P, C], F32, tag="tt", name="tt%d" % i)
             live["tt%d" % i] = tt
             nc.scalar.activation(out=tt[:], in_=live["u%d" % i][:], func=ACTF.Copy, scale=rs[:, i:i + 1])
+            give("u%d" % i)
 
-        def out_transposes(i):
-            v = bank(4 + i % 4, [P, 4, P], F32, "v%d" % i)
-            live["v%d" % i] = v
+        def tall_transposes(i):
+            v = take("v%d" % i, [P, 4, P], F32)
             for j in range(4):
                 nc.tensor.transpose(v[:, j, :], live["tt%d" % i][:, j * P:(j + 1) * P], ident_f[:])
 
-        def add_x(i):
-            for n, (a, b) in enumerate(STORES):
-                if a <= i < b:
-                    nc.vector.scalar_tensor_tensor(
-                        out=og[n][:, :, (i - a) * P:(i - a + 1) * P], in0=live["v%d" % i][:],
-                        scalar=gam[:, 0:1], in1=xr[i // 4][:, :, (i % 4) * P:(i % 4 + 1) * P],
-                        op0=ALU.mult, op1=ALU.add,
-                    )
-                    if i == b - 1:
-                        nc.sync.dma_start(out=out_v[:, :, a * P:b * P], in_=og[n][:])
+        def tall_add(i):
+            o = work.tile([P, 4, P], F32, tag="ot", bufs=8, name="ot%d" % i)
+            cols = slice((i % 4) * P, (i % 4 + 1) * P)
+            nc.vector.tensor_tensor(out=o[:], in0=live["v%d" % i][:], in1=xr[i // 4][:, :, cols], op=ALU.add)
+            give("v%d" % i)
+            nc.sync.dma_start(out=out_v[:, :, i * P:(i + 1) * P], in_=o[:])
 
-        def pair(j):
-            return [i for i in (2 * j, 2 * j + 1) if 0 <= i < NT]
 
         for t in range(4):
             for f in range(4):
                 regroup_x(t, f)
 
-        for i in range(NT):
+        LEAD = 5
+        for i in range(LEAD):
             scores(i)
-            if i == 3:
-                w3_transposes()
-            row_max(i)
-            exponent(i)
-            if i == 6:
-                w3_regroup()
-            if i == 9:
-                nc.vector.quantize_mx(out=w3q[:].bitcast(FP8X4), scales=w3s[:], in_=w3g[:])
-            if i == 12:
+        for a in range(NT):
+            if 12 <= a < 15:
+                pool_max(0, a - 11)
+            row_max(a)
+            exponent(a)
+            if a + LEAD < NT:
+                scores(a + LEAD)
+            if a == 2:
+                nc.gpsimd.tensor_copy(out=gam[:], in_=gam_bf[:])
+            if a == 4:
+                w3_transposes(0)
+                w3_transposes(1)
+            if a == 6:
+                w3_regroup(0)
+            if a == 7:
+                w3_regroup(1)
+            if a == 8:
                 quantise_x(0)
-            if i == 15:
+            if a == 9:
+                w3_quantise()
+                pixel_product(0, 0)
+                pixel_product(0, 1)
+            if a == 10:
+                sum_product(0)
+                pool_start(0)
+                pixel_product(0, 2)
+            if a == 11:
                 quantise_x(1)
-
-        for t in range(4):
-            for f in range(4):
-                live["ph%d" % f] = bank((6, 7, 4, 5)[f], [P, C], F32, "c3_%d_%d" % (t, f))
-                mx_first(live["ph%d" % f], t, f, True, True)
-            if t + 2 < 4:
-                quantise_x(t + 2)
-            pool_start(t)
-            live["sum"] = bank(t % 2, [P, C], F32, "sum%d" % t)
-            for f in range(4):
-                mx_first(live["sum"], t, f, f == 0, f == 3)
-            for i in pair(t - 2):
-                e_quantise(i)
+                pixel_product(0, 3)
+            if a == 12:
+                pool_mean(0)
+                e_transposes(0)
+                pixel_product(1, 0)
+            if a == 13:
+                e_regroup(0)
+                pixel_product(1, 1)
+                e_transposes(1)
+            if a == 14:
+                pool_end(0)
+                pool_start(1)
+                pixel_product(1, 2)
+                sum_product(1)
+            if a == 15:
+                quantise_x(2)
+                e_transposes(2)
+                pixel_product(1, 3)
+        e_regroup(1)
+        for t in range(1, 4):
+            if t < 3:
+                pixel_product(t + 1, 0)
             pool_max(t, 1)
-            for i in pair(t - 1):
-                e_regroup(i, "scalar")
-            for i in pair(t):
-                e_transposes(i, 2 + i % 2)
-            pool_mean(t)
+            e_regroup(t + 1)
+            if t < 3:
+                pixel_product(t + 1, 1)
+                pool_start(t + 1)
+                pool_mean(t)
             pool_max(t, 2)
+            if t == 1:
+                e_quantise(0)
+                quantise_x(3)
+            elif t == 2:
+                e_quantise(1)
+                e_quantise(2)
+            else:
+                e_quantise(3)
+            if t < 3:
+                pixel_product(t + 1, 2)
+                sum_product(t + 1)
+                e_transposes(t + 2)
             pool_max(t, 3)
-            pool_end(t)
-
-        nc.vector.reciprocal(out=rs[:], in_=sig[:])
-        for i in range(8, NT + 2):
-            if i < NT:
-                e_transposes(i, (2, 3, 6, 7, 4, 5)[i % 6])
-            e_regroup(i - 2, "scalar" if i % 2 == 0 else "vector")
-            if i < NT:
-                e_quantise(i - 4)
-            if i == 12:
-                nc.vector.quantize_mx(
-                    out=c3q[:].bitcast(FP8X4), scales=c3s[:], in_=c3g[:].rearrange("p c t -> p (c t)")
-                )
-
-        for e in range(NT // 2 + 3):
-            for i in pair(e + 1):
-                if i >= 12:
-                    e_quantise(i)
-            for i in pair(e - 1):
-                normalise(i)
-            for i in pair(e - 2):
-                out_transposes(i)
-            for i in pair(e):
-                second_product(i)
-            for i in pair(e - 3):
-                add_x(i)
+            if t == 1:
+                norm()
+            if t < 3:
+                pixel_product(t + 1, 3)
+                pool_end(t)
+        e_transposes(5)
+        norm_transposes(0)
+        norm_transposes(1)
+        e_transposes(6)
+        e_transposes(7)
+        norm_copy(0)
+        for half in range(2):
+            pool_end_last(3, half)
+        e_regroup(5)
+        c3_interleave(0, "vector")
+        c3_interleave(1, "vector")
+        c3_interleave(2, "scalar")
+        c3_quantise(0)
+        c3_quantise(1)
+        norm_copy(1)
+        c3_interleave(3, "scalar")
+        e_quantise(4)
+        c3_quantise(2)
+        c3_quantise(3)
+        e_quantise(5)
+        e_regroup(6)
+        e_regroup(7)
+        wide = [("w", (g, j)) for j in range(4) for g in range(WIDE)]
+        tall = [("t", i) for i in range(4 * WIDE, NT)]
+        seq = wide[:5] + tall[:2] + wide[5:6] + tall[2:4] + wide[6:7] + tall[4:6] + wide[7:] + tall[6:]
+        WLEAD, TLEAD, VLEAD = 3, 5, 2
+        for n in range(-TLEAD, len(seq) + 3):
+            for kind, lead in (("t", TLEAD), ("w", WLEAD)):
+                if 0 <= n + lead < len(seq) and seq[n + lead][0] == kind:
+                    a = seq[n + lead][1]
+                    if kind == "w":
+                        wide_product(*a)
+                    else:
+                        tall_product(a)
+                        tall_normalise(a)
+            if n in (0, 1):
+                e_quantise(n + 6)
+            if 0 <= n + VLEAD < len(seq) and seq[n + VLEAD][0] == "t" and seq[n + VLEAD][1] % 2 == 0:
+                tall_transposes(seq[n + VLEAD][1])
+                tall_transposes(seq[n + VLEAD][1] + 1)
+            if 0 <= n < len(seq):
+                kind, a = seq[n]
+                if kind == "w":
+                    wide_normalise(*a)
+                    wide_add(*a)
+                else:
+                    tall_add(a)
+            if 0 <= n - 3 and seq[n - 3][0] == "w":
+                wide_store(*seq[n - 3][1])

@@ -72,7 +72,7 @@ def tile_selfspatialattentionmodule_pb_kernel(tc, x, c2, c1p, W3, gamma, out):
         load_c2(3)
         load_x(2)
         load_x(3)
-        nc.scalar.dma_start(out=gam_bf[:], in_=gamma.partition_broadcast(P))
+        nc.sync.dma_start(out=gam_bf[:], in_=gamma.partition_broadcast(P))
 
         warm = keep.tile([P, 1], F32, name="warm")
         nc.vector.memset(warm[:], 0.0)
@@ -315,8 +315,6 @@ def tile_selfspatialattentionmodule_pb_kernel(tc, x, c2, c1p, W3, gamma, out):
             exponent(a)
             if a + LEAD < NT:
                 scores(a + LEAD)
-            if a == 2:
-                nc.gpsimd.tensor_copy(out=gam[:], in_=gam_bf[:])
             if a == 4:
                 w3_transposes(0)
                 w3_transposes(1)
@@ -379,6 +377,7 @@ def tile_selfspatialattentionmodule_pb_kernel(tc, x, c2, c1p, W3, gamma, out):
                 e_transposes(t + 2)
             pool_max(t, 3)
             if t == 1:
+                nc.gpsimd.tensor_copy(out=gam[:], in_=gam_bf[:])
                 norm()
             if t < 3:
                 pixel_product(t + 1, 3)

@@ -105,11 +105,12 @@ def tile_selfspatialattentionmodule_pb_kernel(tc, x, c2, c1p, W3, gamma, out):
         rs = keep.tile([P, NT], F32, name="rs")
         rsb = keep.tile([P, WIDE, 512], F32, name="rsb")
 
-        def regroup_x(t, f):
-            src = xr[t][:].rearrange("p j (a dh jj dw) -> p dh dw a jj j", a=8, dh=2, jj=16, dw=2)
-            dst = xg[t][:, f].rearrange("p (a jj) j -> p a jj j", a=8)
+        def regroup_x(t, part):
+            dh, half = part // 2, part % 2
+            src = xr[t][:].rearrange("p j (b a dh jj dw) -> p b dh a jj dw j", b=2, a=4, dh=2, jj=16, dw=2)
+            dst = xg[t][:].rearrange("p (dh dw) (b a jj) j -> p b dh a jj dw j", dh=2, b=2, a=4)
             nc.gpsimd.tensor_scalar(
-                out=dst, in0=src[:, f // 2, f % 2], scalar1=1.0, scalar2=0.0, op0=ALU.mult, op1=ALU.add
+                out=dst[:, half, dh], in0=src[:, half, dh], scalar1=1.0, scalar2=0.0, op0=ALU.mult, op1=ALU.add
             )
 
         def quantise_x(t):

@@ -18,6 +18,7 @@ M = 512
 NPIX = 2048
 NT = NPIX // P
 NPAIR = NT // 2
+TALL_STORES = ((8, 10), (10, 12), (12, 14), (14, 16))
 WARM = 4
 VECTOR_ADDS = ((1, 3),)
 WIDE = 2
@@ -156,9 +157,13 @@ def tile_selfspatialattentionmodule_pb_kernel(tc, x, c2, c1p, W3, gamma, out):
             give("ph%d0" % t)
             live["m%d" % t] = m
 
-        def pool_max(t, f):
+        def pool_max(t, f, parts=1):
             m = work.tile([P, C], F32, tag="m", bufs=8, name="m_%d_%d" % (t, f))
-            nc.vector.tensor_tensor(out=m[:], in0=live["m%d" % t][:], in1=live["ph%d%d" % (t, f)][:], op=ALU.max)
+            for h in range(parts):
+                cols = slice(h * C // parts, (h + 1) * C // parts)
+                nc.vector.tensor_tensor(
+                    out=m[:, cols], in0=live["m%d" % t][:, cols], in1=live["ph%d%d" % (t, f)][:, cols], op=ALU.max
+                )
             live["m%d" % t] = m
             give("ph%d%d" % (t, f))
 
@@ -295,11 +300,17 @@ def tile_selfspatialattentionmodule_pb_kernel(tc, x, c2, c1p, W3, gamma, out):
                 nc.tensor.transpose(v[:, j, :], live["tt%d" % i][:, j * P:(j + 1) * P], ident_f[:])
 
         def tall_add(i):
-            o = work.tile([P, 4, P], F32, tag="ot", bufs=8, name="ot%d" % i)
+            a, b = [g for g in TALL_STORES if g[0] <= i < g[1]][0]
+            if i == a:
+                live["ot%d" % a] = keep.tile([P, 4, (b - a) * P], F32, name="ot%d" % a)
+            o = live["ot%d" % a]
             cols = slice((i % 4) * P, (i % 4 + 1) * P)
-            nc.vector.tensor_tensor(out=o[:], in0=live["v%d" % i][:], in1=xr[i // 4][:, :, cols], op=ALU.add)
+            nc.vector.tensor_tensor(
+                out=o[:, :, (i - a) * P:(i - a + 1) * P], in0=live["v%d" % i][:], in1=xr[i // 4][:, :, cols], op=ALU.add
+            )
             give("v%d" % i)
-            nc.sync.dma_start(out=out_v[:, :, i * P:(i + 1) * P], in_=o[:])
+            if i == b - 1:
+                nc.sync.dma_start(out=out_v[:, :, a * P:b * P], in_=o[:])
 
 
         for t in range(4):

@@ -85,7 +85,8 @@ def tile_selfspatialattentionmodule_pb_kernel(tc, x, c2, c1p, W3, gamma, out):
             nc.tensor.matmul(out=wb[:], lhsT=idle[:, 0:P], rhs=idle[:], start=True, stop=True)
         ident_f = keep.tile([P, P], F32, name="ident_f")
         make_identity(nc, ident_f[:])
-        gam = keep.tile([P, 1], F32, name="gam")
+        first_sum = keep.tile([P, 1], F32, name="first_sum")
+        nc.gpsimd.tensor_tensor(out=first_sum[:], in0=ident_f[:, 0:1], in1=ident_f[:, 1:2], op=ALU.add)
 
         w3g = keep.tile([P, 4 * C], BF16, name="w3g", align_bytes=64)
         w3q = keep.tile([P, C], U32, name="w3q", align_bytes=64)
@@ -97,7 +98,7 @@ def tile_selfspatialattentionmodule_pb_kernel(tc, x, c2, c1p, W3, gamma, out):
         c3g = [keep.tile([P, P, 4], BF16, name="c3g%d" % j, align_bytes=64) for j in range(4)]
         c3q = keep.tile([P, C], U32, name="c3q", align_bytes=64)
         c3s = keep.tile([P, C], U8, name="c3s", align_bytes=64)
-        eg = [keep.tile([P, 2, P, 4], BF16, name="eg%d" % k, align_bytes=64) for k in range(NPAIR)]
+        eg = [keep.tile([P, 4, P, 4], BF16, name="eg%d" % g, align_bytes=64) for g in range(4)]
         eq = [keep.tile([P, 512], U32, name="eq%d" % g, align_bytes=64) for g in range(4)]
         es = [keep.tile([P, 512], U8, name="es%d" % g, align_bytes=64) for g in range(4)]
         nmx = keep.tile([P, NT], F32, name="nmx")
@@ -230,23 +231,21 @@ def tile_selfspatialattentionmodule_pb_kernel(tc, x, c2, c1p, W3, gamma, out):
                     nc.tensor.transpose(et[:, i, u, :], words[:, u * P:(u + 1) * P], ident_f[:])
 
         def e_regroup(k):
-            dst = eg[k][:].rearrange("p i n t -> p (i n t)").bitcast(F32)
+            dst = eg[k // 2][:, k % 2 * 2:k % 2 * 2 + 2].rearrange("p i n t -> p (i n t)").bitcast(F32)
             nc.scalar.copy(
                 out=dst.rearrange("p (i n u) -> p i n u", i=2, u=2),
                 in_=live["et%d" % k][:].rearrange("p i u n -> p i n u"),
             )
             give("et%d" % k)
 
-        def e_quantise(k):
-            cols = slice((k % 2) * 2 * P, (k % 2 + 1) * 2 * P)
+        def e_quantise(g):
             nc.vector.quantize_mx(
-                out=eq[k // 2][:, cols].bitcast(FP8X4), scales=es[k // 2][:, cols],
-                in_=eg[k][:].rearrange("p i n t -> p (i n t)"),
+                out=eq[g][:].bitcast(FP8X4), scales=es[g][:], in_=eg[g][:].rearrange("p i n t -> p (i n t)")
             )
 
         def norm():
             nc.vector.reciprocal(out=ri[:], in_=sig[:])
-            nc.gpsimd.tensor_scalar(out=rs[:], in0=ri[:], scalar1=gam[:, 0:1], scalar2=0.0, op0=ALU.mult, op1=ALU.add)
+            nc.gpsimd.tensor_scalar(out=rs[:], in0=ri[:], scalar1=gam_bf[:, 0:1], scalar2=None, op0=ALU.mult)
 
         def norm_transposes(g):
             r = take("rb%d" % g, [P, 4, P], F32)
@@ -327,12 +326,12 @@ def tile_selfspatialattentionmodule_pb_kernel(tc, x, c2, c1p, W3, gamma, out):
             exponent(a)
             if a + LEAD < NT:
                 scores(a + LEAD)
-            if a == 4:
+            if a == 3:
                 w3_transposes(0)
                 w3_transposes(1)
-            if a == 6:
+            if a == 5:
                 w3_regroup(0)
-            if a == 7:
+            if a == 6:
                 w3_regroup(1)
             if a == 8:
                 quantise_x(0)
@@ -341,9 +340,9 @@ def tile_selfspatialattentionmodule_pb_kernel(tc, x, c2, c1p, W3, gamma, out):
                 pixel_product(0, 0)
                 pixel_product(0, 1)
             if a == 10:
-                sum_product(0)
-                pool_start(0)
                 pixel_product(0, 2)
+                pool_start(0)
+                sum_product(0)
             if a == 11:
                 quantise_x(1)
                 pixel_product(0, 3)
@@ -376,30 +375,26 @@ def tile_selfspatialattentionmodule_pb_kernel(tc, x, c2, c1p, W3, gamma, out):
                 pool_mean(t)
             pool_max(t, 2)
             if t == 1:
-                e_quantise(0)
                 quantise_x(3)
-            elif t == 2:
-                e_quantise(1)
-                e_quantise(2)
             else:
-                e_quantise(3)
+                e_quantise(t - 2)
             if t < 3:
                 pixel_product(t + 1, 2)
                 sum_product(t + 1)
                 e_transposes(t + 2)
             pool_max(t, 3)
             if t == 1:
-                nc.gpsimd.tensor_copy(out=gam[:], in_=gam_bf[:])
                 norm()
             if t < 3:
                 pixel_product(t + 1, 3)
                 pool_end(t)
-        e_transposes(5)
         norm_transposes(0)
         norm_transposes(1)
+        e_transposes(5)
         e_transposes(6)
         e_transposes(7)
         norm_copy(0)
+        norm_copy(1)
         for half in range(2):
             pool_end_last(3, half)
         e_regroup(5)
@@ -408,19 +403,19 @@ def tile_selfspatialattentionmodule_pb_kernel(tc, x, c2, c1p, W3, gamma, out):
         c3_interleave(2, "scalar")
         c3_quantise(0)
         c3_quantise(1)
-        norm_copy(1)
         c3_interleave(3, "scalar")
-        e_quantise(4)
+        e_quantise(2)
         c3_quantise(2)
         c3_quantise(3)
-        e_quantise(5)
         e_regroup(6)
         e_regroup(7)
         wide = [("w", (g, j)) for j in range(4) for g in range(WIDE)]
         tall = [("t", i) for i in range(4 * WIDE, NT)]
         seq = wide[:5] + tall[:2] + wide[5:6] + tall[2:4] + wide[6:7] + tall[4:6] + wide[7:] + tall[6:]
-        WLEAD, TLEAD, VLEAD = 3, 5, 2
-        for n in range(-TLEAD, len(seq) + 3):
+        WLEAD, TLEAD, VLEAD, SLAG = 3, 5, 2, 4
+        for n in range(-TLEAD, len(seq) + SLAG):
+            if 0 <= n - SLAG and seq[n - SLAG][0] == "w" and seq[n - SLAG][1] not in VECTOR_ADDS:
+                wide_store(*seq[n - SLAG][1])
             for kind, lead in (("t", TLEAD), ("w", WLEAD)):
                 if 0 <= n + lead < len(seq) and seq[n + lead][0] == kind:
                     a = seq[n + lead][1]
@@ -429,8 +424,8 @@ def tile_selfspatialattentionmodule_pb_kernel(tc, x, c2, c1p, W3, gamma, out):
                     else:
                         tall_product(a)
                         tall_normalise(a)
-            if n in (0, 1):
-                e_quantise(n + 6)
+            if n == 1:
+                e_quantise(3)
             if 0 <= n + VLEAD < len(seq) and seq[n + VLEAD][0] == "t" and seq[n + VLEAD][1] % 2 == 0:
                 tall_transposes(seq[n + VLEAD][1])
                 tall_transposes(seq[n + VLEAD][1] + 1)
@@ -439,7 +434,7 @@ def tile_selfspatialattentionmodule_pb_kernel(tc, x, c2, c1p, W3, gamma, out):
                 if kind == "w":
                     wide_normalise(*a)
                     wide_add(*a)
+                    if a in VECTOR_ADDS:
+                        wide_store(*a)
                 else:
                     tall_add(a)
-            if 0 <= n - 3 and seq[n - 3][0] == "w":
-                wide_store(*seq[n - 3][1])

from contextlib import ExitStack

import concourse.mybir as mybir
from concourse.masks import make_identity

F32 = mybir.dt.float32
BF16 = mybir.dt.bfloat16
U32 = mybir.dt.uint32
U8 = mybir.dt.uint8
FP8X4 = mybir.dt.float8_e4m3fn_x4
ALU = mybir.AluOpType
ACTF = mybir.ActivationFunctionType
AX = mybir.AxisListType

P = 128
C = 512
M = 512
NPIX = 2048
NT = NPIX // P
NPAIR = NT // 2
TALL_STORES = ((8, 10), (10, 12), (12, 14), (14, 16))
WARM = 4
VECTOR_ADDS = ((1, 3),)
WIDE = 2
FLOPS = 2 * (C * C * NPIX + NPIX * M * 256 + C * M * NPIX)


def tile_selfspatialattentionmodule_pb_kernel(tc, x, c2, c1p, W3, gamma, out):
    nc = tc.nc
    x_v = x[0].rearrange("(p j) h w -> p j (h w)", j=4)
    out_v = out[0].rearrange("(p j) h w -> p j (h w)", j=4)
    c2_v = c2[0].rearrange("(p g) h w -> p g (h w)", g=2)
    c1_v = c1p[0].rearrange("(p g) h w -> p g (h w)", g=2)
    w3_v = W3.rearrange("(p j) k -> p (j k)", j=4)

    with ExitStack() as ctx:
        keep = ctx.enter_context(tc.tile_pool(name="keep", bufs=1))
        work = ctx.enter_context(tc.tile_pool(name="work", bufs=4))
        psum = ctx.enter_context(tc.psum_pool(name="psum", bufs=1))
        ctx.enter_context(tc.manual_schedule())
        live = {}
        free = list(range(8))
        held = {}

        def take(name, shape, dtype):
            held[name] = free.pop(0)
            live[name] = psum.tile(shape, dtype, tag="bank%d" % held[name], name=name)
            return live[name]

        def give(name):
            free.append(held[name])

        c1s = keep.tile([P, 2, M], BF16, name="c1s")
        c2s = [keep.tile([P, 2, 512], BF16, name="c2s%d" % g) for g in range(4)]
        xr = [keep.tile([P, 4, 512], BF16, name="xr%d" % g) for g in range(4)]
        w3r = keep.tile([P, 4 * C], BF16, name="w3r")
        gam_bf = keep.tile([P, 1], BF16, name="gam_bf")

        def load_c2(g):
            nc.sync.dma_start(out=c2s[g][:], in_=c2_v[:, :, g * 512:(g + 1) * 512])

        def load_x(g):
            nc.sync.dma_start(out=xr[g][:], in_=x_v[:, :, g * 512:(g + 1) * 512])

        for h in range(2):
            nc.sync.dma_start(out=c1s[:, h, :], in_=c1_v[:, h, :])
            nc.sync.dma_start(out=c2s[0][:, h, :], in_=c2_v[:, h, 0:512])
        load_x(0)
        load_c2(1)
        nc.sync.dma_start(out=w3r[:], in_=w3_v)
        load_c2(2)
        load_x(1)
        load_c2(3)
        load_x(2)
        load_x(3)
        nc.sync.dma_start(out=gam_bf[:], in_=gamma.partition_broadcast(P))

        warm = keep.tile([P, 1], F32, name="warm")
        nc.vector.memset(warm[:], 0.0)
        nc.scalar.activation(out=warm[:], in_=warm[:], func=ACTF.Exp)
        idle = keep.tile([P, 512], BF16, name="idle")
        nc.vector.memset(idle[:], 0.0)
        wb = psum.tile([P, 512], F32, tag="bank7", name="wb")
        for n in range(WARM):
            nc.tensor.matmul(out=wb[:], lhsT=idle[:, 0:P], rhs=idle[:], start=True, stop=True)
        ident_f = keep.tile([P, P], F32, name="ident_f")
        make_identity(nc, ident_f[:])
        first_sum = keep.tile([P, 1], F32, name="first_sum")
        nc.gpsimd.tensor_tensor(out=first_sum[:], in0=ident_f[:, 0:1], in1=ident_f[:, 1:2], op=ALU.add)

        w3g = keep.tile([P, 4 * C], BF16, name="w3g", align_bytes=64)
        w3q = keep.tile([P, C], U32, name="w3q", align_bytes=64)
        w3s = keep.tile([P, C], U8, name="w3s", align_bytes=64)
        xg = [keep.tile([P, 4, P, 4], BF16, name="xg%d" % t, align_bytes=64) for t in range(4)]
        xq = [keep.tile([P, 4 * P], U32, name="xq%d" % t, align_bytes=64) for t in range(4)]
        xs = [keep.tile([P, 4 * P], U8, name="xs%d" % t, align_bytes=64) for t in range(4)]
        c3w = keep.tile([P, 4, C], BF16, name="c3w")
        c3g = [keep.tile([P, P, 4], BF16, name="c3g%d" % j, align_bytes=64) for j in range(4)]
        c3q = keep.tile([P, C], U32, name="c3q", align_bytes=64)
        c3s = keep.tile([P, C], U8, name="c3s", align_bytes=64)
        eg = [keep.tile([P, 4, P, 4], BF16, name="eg%d" % g, align_bytes=64) for g in range(4)]
        eq = [keep.tile([P, 512], U32, name="eq%d" % g, align_bytes=64) for g in range(4)]
        es = [keep.tile([P, 512], U8, name="es%d" % g, align_bytes=64) for g in range(4)]
        nmx = keep.tile([P, NT], F32, name="nmx")
        sig = keep.tile([P, NT], F32, name="sig")
        ri = keep.tile([P, NT], F32, name="ri")
        rs = keep.tile([P, NT], F32, name="rs")
        rsb = keep.tile([P, WIDE, 512], F32, name="rsb")

        def regroup_x(t, part):
            dh, half = part // 2, part % 2
            src = xr[t][:].rearrange("p j (b a dh jj dw) -> p b dh a jj dw j", b=2, a=4, dh=2, jj=16, dw=2)
            dst = xg[t][:].rearrange("p (dh dw) (b a jj) j -> p b dh a jj dw j", dh=2, b=2, a=4)
            nc.gpsimd.tensor_scalar(
                out=dst[:, half, dh], in0=src[:, half, dh], scalar1=1.0, scalar2=0.0, op0=ALU.mult, op1=ALU.add
            )

        def quantise_x(t):
            nc.vector.quantize_mx(
                out=xq[t][:].bitcast(FP8X4), scales=xs[t][:], in_=xg[t][:].rearrange("p f c j -> p (f c j)")
            )

        def w3_transposes(half):
            w3w = w3r[:].bitcast(F32).rearrange("p (j w u) -> p j u w", j=4, w=P, u=2)
            wt = take("wt%d" % half, [P, 2, 2, P], F32)
            for jj in range(2):
                for u in range(2):
                    nc.tensor.transpose(wt[:, jj, u, :], w3w[:, 2 * half + jj, u, :], ident_f[:])

        def w3_regroup(half):
            w3gw = w3g[:].bitcast(F32).rearrange("p (j c u) -> p j c u", j=4, c=P, u=2)
            nc.scalar.copy(
                out=w3gw[:, 2 * half:2 * half + 2], in_=live["wt%d" % half][:].rearrange("p j u c -> p j c u")
            )
            give("wt%d" % half)

        def w3_quantise():
            nc.vector.quantize_mx(out=w3q[:].bitcast(FP8X4), scales=w3s[:], in_=w3g[:])

        def mx_first(dst, t, f, first, last):
            cols = slice(f * P, (f + 1) * P)
            nc.tensor.matmul_mx(
                out=dst[:], lhsT=xq[t][:, cols].bitcast(FP8X4), lhsT_scale=xs[t][:, cols],
                rhs=w3q[:].bitcast(FP8X4), rhs_scale=w3s[:], start=first, stop=last,
            )

        def pixel_product(t, f):
            mx_first(take("ph%d%d" % (t, f), [P, C], F32), t, f, True, True)

        def sum_product(t):
            total = take("sum%d" % t, [P, C], F32)
            for f in range(4):
                mx_first(total, t, f, f == 0, f == 3)

        def pool_start(t):
            m = work.tile([P, C], F32, tag="m", bufs=8, name="m_%d_0" % t)
            nc.scalar.copy(out=m[:], in_=live["ph%d0" % t][:])
            give("ph%d0" % t)
            live["m%d" % t] = m

        def pool_max(t, f, parts=1):
            m = work.tile([P, C], F32, tag="m", bufs=8, name="m_%d_%d" % (t, f))
            for h in range(parts):
                cols = slice(h * C // parts, (h + 1) * C // parts)
                nc.vector.tensor_tensor(
                    out=m[:, cols], in0=live["m%d" % t][:, cols], in1=live["ph%d%d" % (t, f)][:, cols], op=ALU.max
                )
            live["m%d" % t] = m
            give("ph%d%d" % (t, f))

        def pool_mean(t):
            smq = work.tile([P, C], F32, tag="smq", name="smq%d" % t)
            nc.scalar.activation(out=smq[:], in_=live["sum%d" % t][:], func=ACTF.Copy, scale=0.25)
            live["smq%d" % t] = smq
            give("sum%d" % t)

        def pool_end(t):
            nc.gpsimd.tensor_tensor(out=c3w[:, t, :], in0=live["m%d" % t][:], in1=live["smq%d" % t][:], op=ALU.add)

        def pool_end_last(t, half):
            cols = slice(half * 256, (half + 1) * 256)
            nc.vector.scalar_tensor_tensor(
                out=c3w[:, t, cols], in0=live["sum%d" % t][:, cols], scalar=0.25, in1=live["m%d" % t][:, cols],
                op0=ALU.mult, op1=ALU.add,
            )
            if half == 1:
                give("sum%d" % t)

        def c3_interleave(j, eng):
            src = c3w[:, :, j * P:(j + 1) * P].rearrange("p t c -> p c t")
            if eng == "scalar":
                nc.scalar.copy(out=c3g[j][:], in_=src)
            elif eng == "gpsimd":
                nc.gpsimd.tensor_scalar(out=c3g[j][:], in0=src, scalar1=1.0, scalar2=0.0, op0=ALU.mult, op1=ALU.add)
            else:
                nc.vector.tensor_copy(out=c3g[j][:], in_=src)

        def c3_quantise(j):
            nc.vector.quantize_mx(
                out=c3q[:, j * P:(j + 1) * P].bitcast(FP8X4), scales=c3s[:, j * P:(j + 1) * P], in_=c3g[j][:].rearrange("p c t -> p (c t)")
            )

        def scores(i):
            s = take("s%d" % i, [P, M], F32)
            for h in range(2):
                nc.tensor.matmul(
                    out=s[:], lhsT=c2s[i // 4][:, h, (i % 4) * P:(i % 4 + 1) * P], rhs=c1s[:, h, :],
                    start=(h == 0), stop=(h == 1),
                )

        def row_max(i):
            nc.vector.tensor_reduce(
                out=nmx[:, i:i + 1], in_=live["s%d" % i][:], axis=AX.X, op=ALU.max, negate=True
            )

        def exponent(i):
            ee = keep.tile([P, M], BF16, name="ee%d" % i)
            live["ee%d" % i] = ee
            nc.scalar.activation(
                out=ee[:].rearrange("p (u q e) -> p u q e", u=2, e=2),
                in_=live["s%d" % i][:].rearrange("p (u e q) -> p u q e", u=2, e=2),
                func=ACTF.Exp, bias=nmx[:, i:i + 1], scale=1.0, accum_out=sig[:, i:i + 1],
            )
            give("s%d" % i)

        def e_transposes(k):
            et = take("et%d" % k, [P, 2, 2, P], F32)
            for i in range(2):
                words = live["ee%d" % (2 * k + i)][:].bitcast(F32)
                for u in range(2):
                    nc.tensor.transpose(et[:, i, u, :], words[:, u * P:(u + 1) * P], ident_f[:])

        def e_regroup(k):
            dst = eg[k // 2][:, k % 2 * 2:k % 2 * 2 + 2].rearrange("p i n t -> p (i n t)").bitcast(F32)
            nc.scalar.copy(
                out=dst.rearrange("p (i n u) -> p i n u", i=2, u=2),
                in_=live["et%d" % k][:].rearrange("p i u n -> p i n u"),
            )
            give("et%d" % k)

        def e_quantise(g):
            nc.vector.quantize_mx(
                out=eq[g][:].bitcast(FP8X4), scales=es[g][:], in_=eg[g][:].rearrange("p i n t -> p (i n t)")
            )

        def norm():
            nc.vector.reciprocal(out=ri[:], in_=sig[:])
            nc.gpsimd.tensor_scalar(out=rs[:], in0=ri[:], scalar1=gam_bf[:, 0:1], scalar2=None, op0=ALU.mult)

        def norm_transposes(g):
            r = take("rb%d" % g, [P, 4, P], F32)
            for i in range(4):
                col = rs[:, 4 * g + i:4 * g + i + 1]
                nc.tensor.transpose(r[:, i, :], col.to_broadcast([P, P]), ident_f[:])

        def norm_copy(g):
            nc.scalar.copy(out=rsb[:, g, :], in_=live["rb%d" % g][:].rearrange("p i n -> p (i n)"))
            give("rb%d" % g)

        def wide_product(g, j):
            u = take("w%d_%d" % (g, j), [P, 512], F32)
            nc.tensor.matmul_mx(
                out=u[:], lhsT=c3q[:, j * P:(j + 1) * P].bitcast(FP8X4), lhsT_scale=c3s[:, j * P:(j + 1) * P],
                rhs=eq[g][:].bitcast(FP8X4), rhs_scale=es[g][:], start=True, stop=True,
            )

        def wide_normalise(g, j):
            tt = work.tile([P, 512], F32, tag="tw", name="tw%d_%d" % (g, j))
            live["tw%d_%d" % (g, j)] = tt
            nc.vector.tensor_tensor(out=tt[:], in0=live["w%d_%d" % (g, j)][:], in1=rsb[:, g, :], op=ALU.mult)
            give("w%d_%d" % (g, j))

        def wide_add(g, j):
            o = work.tile([P, 512], F32, tag="ow", bufs=8, name="ow%d_%d" % (g, j))
            live["ow%d_%d" % (g, j)] = o
            eng = nc.vector if (g, j) in VECTOR_ADDS else nc.gpsimd
            eng.tensor_tensor(out=o[:], in0=live["tw%d_%d" % (g, j)][:], in1=xr[g][:, j, :], op=ALU.add)

        def wide_store(g, j):
            nc.sync.dma_start(out=out_v[:, j, g * 512:(g + 1) * 512], in_=live["ow%d_%d" % (g, j)][:])

        def tall_product(i):
            u = take("u%d" % i, [P, C], F32)
            cols = slice((i % 4) * P, (i % 4 + 1) * P)
            nc.tensor.matmul_mx(
                out=u[:], lhsT=eq[i // 4][:, cols].bitcast(FP8X4), lhsT_scale=es[i // 4][:, cols],
                rhs=c3q[:].bitcast(FP8X4), rhs_scale=c3s[:], start=True, stop=True,
            )

        def tall_normalise(i):
            tt = work.tile([P, C], F32, tag="tt", name="tt%d" % i)
            live["tt%d" % i] = tt
            nc.scalar.activation(out=tt[:], in_=live["u%d" % i][:], func=ACTF.Copy, scale=rs[:, i:i + 1])
            give("u%d" % i)

        def tall_transposes(i):
            v = take("v%d" % i, [P, 4, P], F32)
            for j in range(4):
                nc.tensor.transpose(v[:, j, :], live["tt%d" % i][:, j * P:(j + 1) * P], ident_f[:])

        def tall_add(i):
            a, b = [g for g in TALL_STORES if g[0] <= i < g[1]][0]
            if i == a:
                live["ot%d" % a] = keep.tile([P, 4, (b - a) * P], F32, name="ot%d" % a)
            o = live["ot%d" % a]
            cols = slice((i % 4) * P, (i % 4 + 1) * P)
            nc.vector.tensor_tensor(
                out=o[:, :, (i - a) * P:(i - a + 1) * P], in0=live["v%d" % i][:], in1=xr[i // 4][:, :, cols], op=ALU.add
            )
            give("v%d" % i)
            if i == b - 1:
                nc.sync.dma_start(out=out_v[:, :, a * P:b * P], in_=o[:])


        for t in range(4):
            for f in range(4):
                regroup_x(t, f)

        LEAD = 5
        for i in range(LEAD):
            scores(i)
        for a in range(NT):
            if 12 <= a < 15:
                pool_max(0, a - 11)
            row_max(a)
            exponent(a)
            if a + LEAD < NT:
                scores(a + LEAD)
            if a == 3:
                w3_transposes(0)
                w3_transposes(1)
            if a == 5:
                w3_regroup(0)
            if a == 6:
                w3_regroup(1)
            if a == 8:
                quantise_x(0)
            if a == 9:
                w3_quantise()
                pixel_product(0, 0)
                pixel_product(0, 1)
            if a == 10:
                pixel_product(0, 2)
                pool_start(0)
                sum_product(0)
            if a == 11:
                quantise_x(1)
                pixel_product(0, 3)
            if a == 12:
                pool_mean(0)
                e_transposes(0)
                pixel_product(1, 0)
            if a == 13:
                e_regroup(0)
                pixel_product(1, 1)
                e_transposes(1)
            if a == 14:
                pool_end(0)
                pool_start(1)
                pixel_product(1, 2)
                sum_product(1)
            if a == 15:
                quantise_x(2)
                e_transposes(2)
                pixel_product(1, 3)
        e_regroup(1)
        for t in range(1, 4):
            if t < 3:
                pixel_product(t + 1, 0)
            pool_max(t, 1)
            e_regroup(t + 1)
            if t < 3:
                pixel_product(t + 1, 1)
                pool_start(t + 1)
                pool_mean(t)
            pool_max(t, 2)
            if t == 1:
                quantise_x(3)
            else:
                e_quantise(t - 2)
            if t < 3:
                pixel_product(t + 1, 2)
                sum_product(t + 1)
                e_transposes(t + 2)
            pool_max(t, 3)
            if t == 1:
                norm()
            if t < 3:
                pixel_product(t + 1, 3)
                pool_end(t)
        norm_transposes(0)
        norm_transposes(1)
        e_transposes(5)
        e_transposes(6)
        e_transposes(7)
        norm_copy(0)
        norm_copy(1)
        for half in range(2):
            pool_end_last(3, half)
        e_regroup(5)
        c3_interleave(0, "vector")
        c3_interleave(1, "vector")
        c3_interleave(2, "scalar")
        c3_quantise(0)
        c3_quantise(1)
        c3_interleave(3, "scalar")
        e_quantise(2)
        c3_quantise(2)
        c3_quantise(3)
        e_regroup(6)
        e_regroup(7)
        wide = [("w", (g, j)) for j in range(4) for g in range(WIDE)]
        tall = [("t", i) for i in range(4 * WIDE, NT)]
        seq = wide[:5] + tall[:2] + wide[5:6] + tall[2:4] + wide[6:7] + tall[4:6] + wide[7:] + tall[6:]
        WLEAD, TLEAD, VLEAD, SLAG = 3, 5, 2, 4
        for n in range(-TLEAD, len(seq) + SLAG):
            if 0 <= n - SLAG and seq[n - SLAG][0] == "w" and seq[n - SLAG][1] not in VECTOR_ADDS:
                wide_store(*seq[n - SLAG][1])
            for kind, lead in (("t", TLEAD), ("w", WLEAD)):
                if 0 <= n + lead < len(seq) and seq[n + lead][0] == kind:
                    a = seq[n + lead][1]
                    if kind == "w":
                        wide_product(*a)
                    else:
                        tall_product(a)
                        tall_normalise(a)
            if n == 1:
                e_quantise(3)
            if 0 <= n + VLEAD < len(seq) and seq[n + VLEAD][0] == "t" and seq[n + VLEAD][1] % 2 == 0:
                tall_transposes(seq[n + VLEAD][1])
                tall_transposes(seq[n + VLEAD][1] + 1)
            if 0 <= n < len(seq):
                kind, a = seq[n]
                if kind == "w":
                    wide_normalise(*a)
                    wide_add(*a)
                    if a in VECTOR_ADDS:
                        wide_store(*a)
                else:
                    tall_add(a)
